import numpy as np
import ml_dtypes


def mxq(x, axis, fmt="e4m3"):
    dtype, down = {"e4m3": (ml_dtypes.float8_e4m3fn, 7), "e5m2": (ml_dtypes.float8_e5m2, 14)}[fmt]
    v = np.moveaxis(np.asarray(x, np.float32).astype(ml_dtypes.bfloat16).astype(np.float64), axis, -1)
    blocks = v.reshape(v.shape[:-1] + (-1, 32))
    amax = np.abs(blocks).max(-1, keepdims=True)
    byte = np.maximum(np.where(amax > 0, np.frexp(amax)[1] - 1 + 127, 0) - down, 1)
    scale = np.exp2(byte - 127.0)
    codes = (blocks / scale).astype(np.float32).astype(dtype).astype(np.float64)
    return np.moveaxis((codes * scale).reshape(v.shape), -1, axis)


WIDE = False


def mx_kscale(k):
    if not WIDE:
        return np.ones(k)
    levels = np.array([10, -10, 5, -5, 0])
    a = np.random.permutation(np.resize(levels, k // 512 * 4)).reshape(k // 512, 4)
    idx = np.arange(k)
    return np.exp2(a[idx // 512, idx % 128 // 32])


BF16 = ml_dtypes.bfloat16


def bf(x):
    return np.asarray(x, np.float32).astype(BF16)


def f64(x):
    return np.asarray(x).astype(np.float64)


E2M1 = np.array([0.0, 0.5, 1.0, 1.5, 2.0, 3.0, 4.0, 6.0, -0.0, -0.5, -1.0, -1.5, -2.0, -3.0, -4.0, -6.0])


def pack_weight(w, fmt):
    k, n = w.shape
    w = f64(bf(w)).reshape(k // 32, 32, n)
    amax = np.abs(w).max(1)
    if fmt == "e4m3":
        byte = np.frexp(amax)[1] - 1 + 127 - 7
    else:
        mant, ex = np.frexp(amax / 6.0)
        byte = np.where(mant > 0.5, ex, ex - 1) + 127
    byte = np.clip(np.where(amax > 0, byte, 1), 1, 254)
    scaled = (w * np.exp2(127.0 - byte)[:, None, :]).reshape(k, n).astype(np.float32)
    by_word = np.ascontiguousarray(scaled.reshape(k // 512, 128, 4, n).transpose(0, 1, 3, 2))
    if fmt == "e4m3":
        words = by_word.astype(ml_dtypes.float8_e4m3fn).view(np.uint8)
    else:
        c = by_word.astype(ml_dtypes.float4_e2m1fn).view(np.uint8) & 0xF
        words = c[..., 0::2] | (c[..., 1::2] << 4)
    return np.ascontiguousarray(words), np.ascontiguousarray(byte.astype(np.uint8).reshape(k // 512, 16, n))


def unpack_weight(words, scales, fmt):
    g, p, n, _ = words.shape
    if fmt == "e4m3":
        vals = np.ascontiguousarray(words).view(ml_dtypes.float8_e4m3fn).astype(np.float64)
    else:
        nib = np.empty((g, p, n, 4), np.uint8)
        nib[..., 0::2] = words & 0xF
        nib[..., 1::2] = words >> 4
        vals = E2M1[nib]
    vals = vals * np.repeat(np.exp2(scales.astype(np.float64) - 127.0), 8, axis=1)[..., None]
    return vals.transpose(0, 1, 3, 2).reshape(g * 512, n)


B, N, D, P, C = 2, 64, 16384, 64, 5
G = 11 + C
O = P * G
OFFSET_MAX = 0.2
SCALE_MAX = 0.02
FMT = "e4m3"


def sigmoid(v):
    return 1.0 / (1.0 + np.exp(-v))


def silu(v):
    return v / (1.0 + np.exp(-v))


def setup_inputs():
    s = mx_kscale(D)
    xyzs = bf(np.random.standard_normal((B, N, 3)) * 0.25)
    latents = bf(np.random.standard_normal((B, N, D)) * s)
    W1_words, W1_scales = pack_weight(np.random.standard_normal((D, O)) / np.sqrt(D) / s[:, None], FMT)
    b1 = bf(np.random.standard_normal(O) * 0.3)
    W2_words, W2_scales = pack_weight(np.random.standard_normal((O, O)) * 2.5 / np.sqrt(O), FMT)
    b2 = bf(np.random.standard_normal(O) * 0.5)
    return {"xyzs": xyzs,
            "latents": latents,
            "W1_words": W1_words,
            "W1_scales": W1_scales,
            "b1": b1,
            "W2_words": W2_words,
            "W2_scales": W2_scales,
            "b2": b2}


def reference(xyzs, latents, W1_words, W1_scales, b1, W2_words, W2_scales, b2):
    xyzs = f64(xyzs)
    h = silu((mxq(f64(latents), 2, "e4m3") @ unpack_weight(W1_words, W1_scales, FMT)) + f64(b1))
    f = (mxq(h, 2, "e4m3") @ unpack_weight(W2_words, W2_scales, FMT)) + f64(b2)
    f = f.reshape(B, N, P, G)
    mean3D = xyzs[:, :, None, :] + sigmoid(f[..., 0:3]) * OFFSET_MAX
    opacity = sigmoid(f[..., 3:4])
    scales = sigmoid(f[..., 4:7]) * SCALE_MAX
    rot = f[..., 7:11]
    rot = rot / np.maximum(np.sqrt(np.sum(rot * rot, axis=-1, keepdims=True)), 1e-12)
    rgb = np.clip(f[..., 11:], -0.5, 0.5) + 0.5
    gaussians = np.concatenate([mean3D, opacity, scales, rot, rgb], axis=-1)
    return gaussians.reshape(B, N * P, G)

@@ -1,0 +1,288 @@
+from contextlib import ExitStack
+
+import concourse.masks as masks
+import concourse.mybir as mybir
+
+F32 = mybir.dt.float32
+BF16 = mybir.dt.bfloat16
+I32 = mybir.dt.int32
+U32 = mybir.dt.uint32
+U8 = mybir.dt.uint8
+FP8X4 = mybir.dt.float8_e4m3fn_x4
+ALU = mybir.AluOpType
+ACT = mybir.ActivationFunctionType
+
+P = 128
+PACK = 4
+K_PASS = P * PACK
+D_IN = 16384
+WIDTH = 1024
+N_PASS = 512
+HALVES = WIDTH // N_PASS
+GROUPS1 = D_IN // K_PASS
+GROUPS2 = WIDTH // K_PASS
+CHANNELS = 16
+GAUSS = WIDTH // CHANNELS
+GAUSS_HALF = GAUSS // HALVES
+
+X_CHUNKS = 4
+X_CHUNK_GROUPS = GROUPS1 // X_CHUNKS
+BANK_GROUPS = 2
+W1_DMA_GROUPS = 2
+W1_BUFS = 12
+SHARED = 4
+QUADS = 4
+
+FLOPS = 2 * P * D_IN * WIDTH + 2 * P * WIDTH * WIDTH
+
+
+def tile_gaussianrenderer_k_kernel(
+    tc, xyzs, latents, W1_words, W1_scales, b1, W2_words, W2_scales, b2, out
+):
+    nc = tc.nc
+
+    x_dram = latents.rearrange("b n d -> (b n) d")
+    xyz_dram = xyzs.rearrange("b n c -> (b n) c")
+    w1_dram = W1_words.rearrange("g p n t -> p g (n t)").bitcast(I32)
+    w2_dram = W2_words.rearrange("g p n t -> p g (n t)").bitcast(I32)
+    w1_scale_dram = W1_scales.bitcast(I32)
+    w2_scale_dram = W2_scales.bitcast(I32)
+    out_dram = out.rearrange("b (n q) c -> (b n) (q c)", q=GAUSS)
+
+    with ExitStack() as ctx:
+        ctx.enter_context(tc.manual_schedule())
+        keep = ctx.enter_context(tc.tile_pool(name="keep", bufs=1))
+        x_pool = ctx.enter_context(tc.tile_pool(name="x", bufs=X_CHUNKS))
+        w1_pool = ctx.enter_context(tc.tile_pool(name="w1", bufs=W1_BUFS))
+        stage = ctx.enter_context(tc.tile_pool(name="stage", bufs=4))
+        tail = ctx.enter_context(tc.tile_pool(name="tail", bufs=2))
+        sums = ctx.enter_context(tc.psum_pool(name="sums", bufs=1))
+        turn = ctx.enter_context(tc.psum_pool(name="turn", bufs=4))
+
+        bias_rows = keep.tile([P, 2 * WIDTH], BF16)
+        nc.vector.memset(bias_rows[:], 0.0)
+        w1_planes = keep.tile([P, GROUPS1 // SHARED, WIDTH], U8, align_bytes=64)
+        nc.vector.memset(w1_planes[:].bitcast(I32), 0)
+        w2_planes = keep.tile([P, WIDTH], U8, align_bytes=64)
+        nc.vector.memset(w2_planes[:].bitcast(I32), 0)
+        ones = keep.tile([P, P], BF16)
+        nc.vector.memset(ones[:], 1.0)
+        ident_f32 = keep.tile([P, P], F32)
+        masks.make_identity(nc, ident_f32[:])
+        ident_bf16 = keep.tile([P, P], BF16)
+        masks.make_identity(nc, ident_bf16[:])
+
+        x_chunks = []
+        chunk_cols = X_CHUNK_GROUPS * K_PASS
+        for c in range(X_CHUNKS):
+            x_sb = x_pool.tile([P, chunk_cols], BF16)
+            nc.sync.dma_start(out=x_sb[:], in_=x_dram[:, c * chunk_cols : (c + 1) * chunk_cols])
+            x_chunks.append(x_sb)
+
+        for s in range(GROUPS1 // SHARED):
+            for quad in range(QUADS):
+                nc.sync.dma_start(
+                    out=w1_planes[32 * quad : 32 * quad + 4 * SHARED, s, :].bitcast(I32),
+                    in_=w1_scale_dram[SHARED * s : SHARED * (s + 1), 4 * quad : 4 * quad + 4, :],
+                )
+        for quad in range(QUADS):
+            nc.sync.dma_start(
+                out=w2_planes[32 * quad : 32 * quad + 4 * GROUPS2, :].bitcast(I32),
+                in_=w2_scale_dram[:, 4 * quad : 4 * quad + 4, :],
+            )
+        w2_words = keep.tile([P, GROUPS2, WIDTH], U32, align_bytes=64)
+        nc.sync.dma_start(out=w2_words[:].bitcast(I32), in_=w2_dram)
+
+        def load_w1(i):
+            w1_sb = w1_pool.tile([P, W1_DMA_GROUPS, WIDTH], U32, align_bytes=64)
+            first = i * W1_DMA_GROUPS
+            nc.sync.dma_start(
+                out=w1_sb[:].bitcast(I32), in_=w1_dram[:, first : first + W1_DMA_GROUPS, :]
+            )
+            return w1_sb
+
+        w1_dmas = GROUPS1 // W1_DMA_GROUPS
+        w1_tiles = [load_w1(i) for i in range(W1_BUFS)]
+
+        nc.scalar.dma_start(out=bias_rows[0:1, 0:WIDTH], in_=b1.unsqueeze(0))
+        nc.scalar.dma_start(out=bias_rows[0:1, WIDTH : 2 * WIDTH], in_=b2.unsqueeze(0))
+        xyz_bf16 = keep.tile([P, 3], BF16)
+        nc.scalar.dma_start(out=xyz_bf16[:], in_=xyz_dram)
+        warm = keep.tile([P, 1], F32)
+        nc.scalar.activation(out=warm[:], in_=ones[:, 0:1], func=ACT.Silu)
+
+        x_codes = keep.tile([P, GROUPS1, P], U32, align_bytes=64)
+        x_scales = keep.tile([P, GROUPS1, P], U8, align_bytes=64)
+        for bank in range(GROUPS1 // BANK_GROUPS):
+            g0 = bank * BANK_GROUPS
+            x_turned = turn.tile([P, BANK_GROUPS * 2, P], F32, tag="turn")
+            for gi in range(BANK_GROUPS):
+                x_words = x_chunks[(g0 + gi) // X_CHUNK_GROUPS][:].bitcast(F32)
+                w0 = ((g0 + gi) % X_CHUNK_GROUPS) * (K_PASS // 2)
+                for u in range(2):
+                    nc.tensor.transpose(
+                        x_turned[:, 2 * gi + u, :],
+                        x_words[:, w0 + u : w0 + K_PASS // 2 : 2],
+                        ident_f32[:],
+                    )
+            x_grouped = stage.tile([P, BANK_GROUPS * K_PASS], BF16, align_bytes=64)
+            nc.scalar.copy(
+                out=x_grouped[:].bitcast(F32).rearrange("p (g r u) -> p g r u", g=BANK_GROUPS, u=2),
+                in_=x_turned[:].rearrange("p (g u) r -> p g r u", u=2),
+            )
+            nc.vector.quantize_mx(
+                out=x_codes[:, g0 : g0 + BANK_GROUPS, :].rearrange("p g r -> p (g r)").bitcast(FP8X4),
+                scales=x_scales[:, g0 : g0 + BANK_GROUPS, :].rearrange("p g r -> p (g r)"),
+                in_=x_grouped[:],
+            )
+
+        b1_all = keep.tile([P, HALVES, PACK, P], F32)
+        b2_all = keep.tile([P, GAUSS, CHANNELS], F32)
+        for half in range(HALVES):
+            spread = turn.tile([P, N_PASS], F32, tag="turn")
+            nc.tensor.matmul(
+                out=spread[:],
+                lhsT=ones[:],
+                rhs=bias_rows[:, half * N_PASS : (half + 1) * N_PASS],
+                start=True,
+                stop=True,
+            )
+            nc.vector.tensor_copy(
+                out=b1_all[:, half, :, :], in_=spread[:].rearrange("p (i t) -> p t i", t=PACK)
+            )
+        for half in range(HALVES):
+            spread = turn.tile([P, N_PASS], F32, tag="turn")
+            nc.tensor.matmul(
+                out=spread[:],
+                lhsT=ones[:],
+                rhs=bias_rows[:, WIDTH + half * N_PASS : WIDTH + (half + 1) * N_PASS],
+                start=True,
+                stop=True,
+            )
+            nc.vector.tensor_copy(
+                out=b2_all[:, half * GAUSS_HALF : (half + 1) * GAUSS_HALF, :],
+                in_=spread[:].rearrange("p (q c) -> p q c", c=CHANNELS),
+            )
+        nc.vector.tensor_scalar_add(out=b2_all[:, :, 11:16], in0=b2_all[:, :, 11:16], scalar1=0.5)
+        xyz_shift = keep.tile([P, 3], F32)
+        nc.vector.tensor_scalar_add(out=xyz_shift[:], in0=xyz_bf16[:], scalar1=0.1)
+        sig_gain = keep.tile([P, 4], F32)
+        nc.vector.tensor_scalar_mul(out=sig_gain[:, 0:1], in0=ones[:, 0:1], scalar1=0.5)
+        nc.vector.tensor_scalar_mul(out=sig_gain[:, 1:4], in0=ones[:, 1:4], scalar1=0.01)
+
+        h_sums = [sums.tile([P, N_PASS], F32, name="h_sum%d" % half) for half in range(HALVES)]
+        for i in range(w1_dmas):
+            for gi in range(W1_DMA_GROUPS):
+                g = i * W1_DMA_GROUPS + gi
+                for half in range(HALVES):
+                    cols = slice(half * N_PASS, (half + 1) * N_PASS)
+                    nc.tensor.matmul_mx(
+                        out=h_sums[half][:],
+                        lhsT=x_codes[:, g, :].bitcast(FP8X4),
+                        lhsT_scale=x_scales[:, g, :],
+                        rhs=w1_tiles[i][:, gi, cols].bitcast(FP8X4),
+                        rhs_scale=w1_planes[4 * (g % SHARED) : P, g // SHARED, cols],
+                        start=(g == 0),
+                        stop=(g == GROUPS1 - 1),
+                    )
+            if i + W1_BUFS < w1_dmas:
+                w1_tiles.append(load_w1(i + W1_BUFS))
+
+        h_codes = keep.tile([P, GROUPS2, P], U32, align_bytes=64)
+        h_scales = keep.tile([P, GROUPS2, P], U8, align_bytes=64)
+        h_turned = []
+        for half in range(HALVES):
+            pre = tail.tile([P, PACK, P], F32)
+            nc.vector.tensor_tensor(
+                out=pre[:],
+                in0=h_sums[half][:].rearrange("p (i t) -> p t i", t=PACK),
+                in1=b1_all[:, half, :, :],
+                op=ALU.add,
+            )
+            h_bf16 = tail.tile([P, PACK, P], BF16)
+            nc.scalar.activation(out=h_bf16[:], in_=pre[:], func=ACT.Silu)
+            turned = turn.tile([P, PACK, P], BF16, tag="turn")
+            for t in range(PACK):
+                nc.tensor.transpose(turned[:, t, :], h_bf16[:, t, :], ident_bf16[:])
+            h_turned.append(turned)
+        for half in range(HALVES):
+            h_grouped = tail.tile([P, P, PACK], BF16, align_bytes=64)
+            if half == 0:
+                nc.vector.tensor_copy(
+                    out=h_grouped[:], in_=h_turned[half][:].rearrange("p t r -> p r t")
+                )
+            else:
+                nc.scalar.copy(out=h_grouped[:], in_=h_turned[half][:].rearrange("p t r -> p r t"))
+            nc.vector.quantize_mx(
+                out=h_codes[:, half, :].bitcast(FP8X4),
+                scales=h_scales[:, half, :],
+                in_=h_grouped[:].rearrange("p r t -> p (r t)"),
+            )
+
+        f_sums = [sums.tile([P, N_PASS], F32, name="f_sum%d" % half) for half in range(HALVES)]
+        for g in range(GROUPS2):
+            for half in range(HALVES):
+                cols = slice(half * N_PASS, (half + 1) * N_PASS)
+                nc.tensor.matmul_mx(
+                    out=f_sums[half][:],
+                    lhsT=h_codes[:, g, :].bitcast(FP8X4),
+                    lhsT_scale=h_scales[:, g, :],
+                    rhs=w2_words[:, g, cols].bitcast(FP8X4),
+                    rhs_scale=w2_planes[4 * g : P, cols],
+                    start=(g == 0),
+                    stop=(g == GROUPS2 - 1),
+                )
+
+        f = keep.tile([P, GAUSS, CHANNELS], F32)
+        squares = keep.tile([P, GAUSS, 4], F32)
+        tanhs = keep.tile([P, GAUSS, 7], F32)
+        for half in range(HALVES):
+            some = slice(half * GAUSS_HALF, (half + 1) * GAUSS_HALF)
+            nc.vector.tensor_tensor(
+                out=f[:, some, :],
+                in0=f_sums[half][:].rearrange("p (q c) -> p q c", c=CHANNELS),
+                in1=b2_all[:, some, :],
+                op=ALU.add,
+            )
+            nc.scalar.activation(out=squares[:, some, :], in_=f[:, some, 7:11], func=ACT.Square)
+            nc.scalar.activation(out=tanhs[:, some, :], in_=f[:, some, 0:7], func=ACT.Tanh, scale=0.5)
+        result = keep.tile([P, GAUSS, CHANNELS], F32)
+        nc.vector.tensor_scalar(
+            out=result[:, :, 11:16],
+            in0=f[:, :, 11:16],
+            scalar1=0.0,
+            scalar2=1.0,
+            op0=ALU.max,
+            op1=ALU.min,
+        )
+        norm_sq = keep.tile([P, GAUSS], F32)
+        nc.vector.tensor_reduce(
+            out=norm_sq[:], in_=squares[:], axis=mybir.AxisListType.X, op=ALU.add
+        )
+        inv_norm = keep.tile([P, GAUSS], F32)
+        nc.scalar.activation(out=inv_norm[:], in_=norm_sq[:], func=ACT.Abs_reciprocal_sqrt)
+        nc.vector.scalar_tensor_tensor(
+            out=result[:, :, 0:3],
+            in0=tanhs[:, :, 0:3],
+            scalar=0.1,
+            in1=xyz_shift[:].unsqueeze(1).to_broadcast([P, GAUSS, 3]),
+            op0=ALU.mult,
+            op1=ALU.add,
+        )
+        nc.vector.scalar_tensor_tensor(
+            out=result[:, :, 3:7],
+            in0=tanhs[:, :, 3:7],
+            scalar=1.0,
+            in1=sig_gain[:].unsqueeze(1).to_broadcast([P, GAUSS, 4]),
+            op0=ALU.add,
+            op1=ALU.mult,
+        )
+        nc.vector.scalar_tensor_tensor(
+            out=result[:, :, 7:11],
+            in0=inv_norm[:].unsqueeze(2).to_broadcast([P, GAUSS, 4]),
+            scalar=1.0e12,
+            in1=f[:, :, 7:11],
+            op0=ALU.min,
+            op1=ALU.mult,
+        )
+        nc.sync.dma_start(out=out_dram, in_=result[:].rearrange("p q c -> p (q c)"))

@@ -45,8 +45,8 @@ def tile_gaussianrenderer_k_kernel(
     xyz_dram = xyzs.rearrange("b n c -> (b n) c")
     w1_dram = W1_words.rearrange("g p n t -> p g (n t)").bitcast(I32)
     w2_dram = W2_words.rearrange("g p n t -> p g (n t)").bitcast(I32)
-    w1_scale_dram = W1_scales.bitcast(I32)
-    w2_scale_dram = W2_scales.bitcast(I32)
+    w1_scale_dram = W1_scales.bitcast(F32)
+    w2_scale_dram = W2_scales.bitcast(F32)
     out_dram = out.rearrange("b (n q) c -> (b n) (q c)", q=GAUSS)
 
     with ExitStack() as ctx:
@@ -81,13 +81,13 @@ def tile_gaussianrenderer_k_kernel(
 
         for s in range(GROUPS1 // SHARED):
             for quad in range(QUADS):
-                nc.sync.dma_start(
-                    out=w1_planes[32 * quad : 32 * quad + 4 * SHARED, s, :].bitcast(I32),
+                nc.gpsimd.dma_start(
+                    out=w1_planes[32 * quad : 32 * quad + 4 * SHARED, s, :].bitcast(F32),
                     in_=w1_scale_dram[SHARED * s : SHARED * (s + 1), 4 * quad : 4 * quad + 4, :],
                 )
         for quad in range(QUADS):
-            nc.sync.dma_start(
-                out=w2_planes[32 * quad : 32 * quad + 4 * GROUPS2, :].bitcast(I32),
+            nc.gpsimd.dma_start(
+                out=w2_planes[32 * quad : 32 * quad + 4 * GROUPS2, :].bitcast(F32),
                 in_=w2_scale_dram[:, 4 * quad : 4 * quad + 4, :],
             )
         w2_words = keep.tile([P, GROUPS2, WIDTH], U32, align_bytes=64)

@@ -45,7 +45,9 @@ def tile_gaussianrenderer_k_kernel(
     xyz_dram = xyzs.rearrange("b n c -> (b n) c")
     w1_dram = W1_words.rearrange("g p n t -> p g (n t)").bitcast(I32)
     w2_dram = W2_words.rearrange("g p n t -> p g (n t)").bitcast(I32)
-    w1_scale_dram = W1_scales.bitcast(F32)
+    w1_scale_dram = W1_scales.bitcast(F32).rearrange(
+        "(s j) (quad r) n -> j r quad s n", j=SHARED, r=4
+    )
     w2_scale_dram = W2_scales.bitcast(F32)
     out_dram = out.rearrange("b (n q) c -> (b n) (q c)", q=GAUSS)
 
@@ -79,11 +81,10 @@ def tile_gaussianrenderer_k_kernel(
             nc.sync.dma_start(out=x_sb[:], in_=x_dram[:, c * chunk_cols : (c + 1) * chunk_cols])
             x_chunks.append(x_sb)
 
-        for s in range(GROUPS1 // SHARED):
-            for quad in range(QUADS):
+        for j in range(SHARED):
+            for r in range(4):
                 nc.gpsimd.dma_start(
-                    out=w1_planes[32 * quad : 32 * quad + 4 * SHARED, s, :].bitcast(F32),
-                    in_=w1_scale_dram[SHARED * s : SHARED * (s + 1), 4 * quad : 4 * quad + 4, :],
+                    out=w1_planes[4 * j + r : P : 32, :, :].bitcast(F32), in_=w1_scale_dram[j, r]
                 )
         for quad in range(QUADS):
             nc.gpsimd.dma_start(

@@ -28,9 +28,10 @@ GAUSS_HALF = GAUSS // HALVES
 X_CHUNKS = 4
 X_CHUNK_GROUPS = GROUPS1 // X_CHUNKS
 BANK_GROUPS = 2
-W1_DMA_GROUPS = 2
-W1_BUFS = 12
+W1_BUFS = 24
 SHARED = 4
+SLOTS = GROUPS1 // SHARED
+SYNC_SLOTS = 2
 QUADS = 4
 
 FLOPS = 2 * P * D_IN * WIDTH + 2 * P * WIDTH * WIDTH
@@ -45,9 +46,6 @@ def tile_gaussianrenderer_k_kernel(
     xyz_dram = xyzs.rearrange("b n c -> (b n) c")
     w1_dram = W1_words.rearrange("g p n t -> p g (n t)").bitcast(I32)
     w2_dram = W2_words.rearrange("g p n t -> p g (n t)").bitcast(I32)
-    w1_scale_dram = W1_scales.bitcast(F32).rearrange(
-        "(s j) (quad r) n -> j r quad s n", j=SHARED, r=4
-    )
     w2_scale_dram = W2_scales.bitcast(F32)
     out_dram = out.rearrange("b (n q) c -> (b n) (q c)", q=GAUSS)
 
@@ -63,7 +61,7 @@ def tile_gaussianrenderer_k_kernel(
 
         bias_rows = keep.tile([P, 2 * WIDTH], BF16)
         nc.vector.memset(bias_rows[:], 0.0)
-        w1_planes = keep.tile([P, GROUPS1 // SHARED, WIDTH], U8, align_bytes=64)
+        w1_planes = keep.tile([P, SLOTS, WIDTH], U8, align_bytes=64)
         nc.vector.memset(w1_planes[:].bitcast(I32), 0)
         w2_planes = keep.tile([P, WIDTH], U8, align_bytes=64)
         nc.vector.memset(w2_planes[:].bitcast(I32), 0)
@@ -81,29 +79,31 @@ def tile_gaussianrenderer_k_kernel(
             nc.sync.dma_start(out=x_sb[:], in_=x_dram[:, c * chunk_cols : (c + 1) * chunk_cols])
             x_chunks.append(x_sb)
 
-        for j in range(SHARED):
-            for r in range(4):
-                nc.gpsimd.dma_start(
-                    out=w1_planes[4 * j + r : P : 32, :, :].bitcast(F32), in_=w1_scale_dram[j, r]
+        def load_plane_slot(queue, view, s):
+            for quad in range(QUADS):
+                queue.dma_start(
+                    out=w1_planes[32 * quad : 32 * quad + 4 * SHARED, s, :].bitcast(view),
+                    in_=W1_scales[
+                        SHARED * s : SHARED * (s + 1), 4 * quad : 4 * quad + 4, :
+                    ].bitcast(view),
                 )
+
+        for s in range(SYNC_SLOTS):
+            load_plane_slot(nc.sync, I32, s)
+        for s in range(SYNC_SLOTS, SLOTS):
+            load_plane_slot(nc.gpsimd, F32, s)
         for quad in range(QUADS):
             nc.gpsimd.dma_start(
                 out=w2_planes[32 * quad : 32 * quad + 4 * GROUPS2, :].bitcast(F32),
                 in_=w2_scale_dram[:, 4 * quad : 4 * quad + 4, :],
             )
-        w2_words = keep.tile([P, GROUPS2, WIDTH], U32, align_bytes=64)
-        nc.sync.dma_start(out=w2_words[:].bitcast(I32), in_=w2_dram)
 
-        def load_w1(i):
-            w1_sb = w1_pool.tile([P, W1_DMA_GROUPS, WIDTH], U32, align_bytes=64)
-            first = i * W1_DMA_GROUPS
-            nc.sync.dma_start(
-                out=w1_sb[:].bitcast(I32), in_=w1_dram[:, first : first + W1_DMA_GROUPS, :]
-            )
+        def load_w1(g):
+            w1_sb = w1_pool.tile([P, WIDTH], U32, align_bytes=64)
+            nc.sync.dma_start(out=w1_sb[:].bitcast(I32), in_=w1_dram[:, g, :])
             return w1_sb
 
-        w1_dmas = GROUPS1 // W1_DMA_GROUPS
-        w1_tiles = [load_w1(i) for i in range(W1_BUFS)]
+        w1_tiles = [load_w1(g) for g in range(W1_BUFS)]
 
         nc.scalar.dma_start(out=bias_rows[0:1, 0:WIDTH], in_=b1.unsqueeze(0))
         nc.scalar.dma_start(out=bias_rows[0:1, WIDTH : 2 * WIDTH], in_=b2.unsqueeze(0))
@@ -172,22 +172,23 @@ def tile_gaussianrenderer_k_kernel(
         nc.vector.tensor_scalar_mul(out=sig_gain[:, 1:4], in0=ones[:, 1:4], scalar1=0.01)
 
         h_sums = [sums.tile([P, N_PASS], F32, name="h_sum%d" % half) for half in range(HALVES)]
-        for i in range(w1_dmas):
-            for gi in range(W1_DMA_GROUPS):
-                g = i * W1_DMA_GROUPS + gi
-                for half in range(HALVES):
-                    cols = slice(half * N_PASS, (half + 1) * N_PASS)
-                    nc.tensor.matmul_mx(
-                        out=h_sums[half][:],
-                        lhsT=x_codes[:, g, :].bitcast(FP8X4),
-                        lhsT_scale=x_scales[:, g, :],
-                        rhs=w1_tiles[i][:, gi, cols].bitcast(FP8X4),
-                        rhs_scale=w1_planes[4 * (g % SHARED) : P, g // SHARED, cols],
-                        start=(g == 0),
-                        stop=(g == GROUPS1 - 1),
-                    )
-            if i + W1_BUFS < w1_dmas:
-                w1_tiles.append(load_w1(i + W1_BUFS))
+        for g in range(GROUPS1):
+            for half in range(HALVES):
+                cols = slice(half * N_PASS, (half + 1) * N_PASS)
+                nc.tensor.matmul_mx(
+                    out=h_sums[half][:],
+                    lhsT=x_codes[:, g, :].bitcast(FP8X4),
+                    lhsT_scale=x_scales[:, g, :],
+                    rhs=w1_tiles[g][:, cols].bitcast(FP8X4),
+                    rhs_scale=w1_planes[4 * (g % SHARED) : P, g // SHARED, cols],
+                    start=(g == 0),
+                    stop=(g == GROUPS1 - 1),
+                )
+            if g + W1_BUFS < GROUPS1:
+                w1_tiles.append(load_w1(g + W1_BUFS))
+        w2_words = keep.tile([P, GROUPS2, WIDTH], U32, align_bytes=64)
+        for g in range(GROUPS2):
+            nc.sync.dma_start(out=w2_words[:, g, :].bitcast(I32), in_=w2_dram[:, g, :])
 
         h_codes = keep.tile([P, GROUPS2, P], U32, align_bytes=64)
         h_scales = keep.tile([P, GROUPS2, P], U8, align_bytes=64)

@@ -28,7 +28,9 @@ GAUSS_HALF = GAUSS // HALVES
 X_CHUNKS = 4
 X_CHUNK_GROUPS = GROUPS1 // X_CHUNKS
 BANK_GROUPS = 2
-W1_BUFS = 24
+LATE = 4
+EARLY = GROUPS1 - LATE
+W1_BUFS = 20
 SHARED = 4
 SLOTS = GROUPS1 // SHARED
 SYNC_SLOTS = 2
@@ -54,6 +56,7 @@ def tile_gaussianrenderer_k_kernel(
         keep = ctx.enter_context(tc.tile_pool(name="keep", bufs=1))
         x_pool = ctx.enter_context(tc.tile_pool(name="x", bufs=X_CHUNKS))
         w1_pool = ctx.enter_context(tc.tile_pool(name="w1", bufs=W1_BUFS))
+        late_pool = ctx.enter_context(tc.tile_pool(name="late", bufs=LATE))
         stage = ctx.enter_context(tc.tile_pool(name="stage", bufs=4))
         tail = ctx.enter_context(tc.tile_pool(name="tail", bufs=2))
         sums = ctx.enter_context(tc.psum_pool(name="sums", bufs=1))
@@ -172,28 +175,42 @@ def tile_gaussianrenderer_k_kernel(
         nc.vector.tensor_scalar_mul(out=sig_gain[:, 1:4], in0=ones[:, 1:4], scalar1=0.01)
 
         h_sums = [sums.tile([P, N_PASS], F32, name="h_sum%d" % half) for half in range(HALVES)]
-        for g in range(GROUPS1):
+        def layer1_pass(g, half):
+            cols = slice(half * N_PASS, (half + 1) * N_PASS)
+            nc.tensor.matmul_mx(
+                out=h_sums[half][:],
+                lhsT=x_codes[:, g, :].bitcast(FP8X4),
+                lhsT_scale=x_scales[:, g, :],
+                rhs=w1_tiles[g][:, cols].bitcast(FP8X4),
+                rhs_scale=w1_planes[4 * (g % SHARED) : P, g // SHARED, cols],
+                start=(g == 0),
+                stop=(g == GROUPS1 - 1),
+            )
+
+        for g in range(EARLY - W1_BUFS):
             for half in range(HALVES):
-                cols = slice(half * N_PASS, (half + 1) * N_PASS)
-                nc.tensor.matmul_mx(
-                    out=h_sums[half][:],
-                    lhsT=x_codes[:, g, :].bitcast(FP8X4),
-                    lhsT_scale=x_scales[:, g, :],
-                    rhs=w1_tiles[g][:, cols].bitcast(FP8X4),
-                    rhs_scale=w1_planes[4 * (g % SHARED) : P, g // SHARED, cols],
-                    start=(g == 0),
-                    stop=(g == GROUPS1 - 1),
-                )
-            if g + W1_BUFS < GROUPS1:
-                w1_tiles.append(load_w1(g + W1_BUFS))
+                layer1_pass(g, half)
+            w1_tiles.append(load_w1(g + W1_BUFS))
+        for g in range(EARLY, GROUPS1):
+            w1_late = late_pool.tile([P, WIDTH], U32, align_bytes=64)
+            w1_tiles.append(w1_late)
+        for half in range(HALVES):
+            cols = slice(half * N_PASS, (half + 1) * N_PASS)
+            for g in range(EARLY, GROUPS1):
+                nc.sync.dma_start(out=w1_tiles[g][:, cols].bitcast(I32), in_=w1_dram[:, g, cols])
         w2_words = keep.tile([P, GROUPS2, WIDTH], U32, align_bytes=64)
         for g in range(GROUPS2):
             nc.sync.dma_start(out=w2_words[:, g, :].bitcast(I32), in_=w2_dram[:, g, :])
+        for g in range(EARLY - W1_BUFS, EARLY):
+            for half in range(HALVES):
+                layer1_pass(g, half)
 
         h_codes = keep.tile([P, GROUPS2, P], U32, align_bytes=64)
         h_scales = keep.tile([P, GROUPS2, P], U8, align_bytes=64)
-        h_turned = []
+        h_halves = []
         for half in range(HALVES):
+            for g in range(EARLY, GROUPS1):
+                layer1_pass(g, half)
             pre = tail.tile([P, PACK, P], F32)
             nc.vector.tensor_tensor(
                 out=pre[:],
@@ -203,9 +220,12 @@ def tile_gaussianrenderer_k_kernel(
             )
             h_bf16 = tail.tile([P, PACK, P], BF16)
             nc.scalar.activation(out=h_bf16[:], in_=pre[:], func=ACT.Silu)
+            h_halves.append(h_bf16)
+        h_turned = []
+        for half in range(HALVES):
             turned = turn.tile([P, PACK, P], BF16, tag="turn")
             for t in range(PACK):
-                nc.tensor.transpose(turned[:, t, :], h_bf16[:, t, :], ident_bf16[:])
+                nc.tensor.transpose(turned[:, t, :], h_halves[half][:, t, :], ident_bf16[:])
             h_turned.append(turned)
         for half in range(HALVES):
             h_grouped = tail.tile([P, P, PACK], BF16, align_bytes=64)
@@ -236,18 +256,25 @@ def tile_gaussianrenderer_k_kernel(
                 )
 
         f = keep.tile([P, GAUSS, CHANNELS], F32)
-        squares = keep.tile([P, GAUSS, 4], F32)
+        for chans in (slice(0, 7), slice(7, CHANNELS)):
+            for half in range(HALVES):
+                some = slice(half * GAUSS_HALF, (half + 1) * GAUSS_HALF)
+                nc.vector.tensor_tensor(
+                    out=f[:, some, chans],
+                    in0=f_sums[half][:].rearrange("p (q c) -> p q c", c=CHANNELS)[:, :, chans],
+                    in1=b2_all[:, some, chans],
+                    op=ALU.add,
+                )
         tanhs = keep.tile([P, GAUSS, 7], F32)
-        for half in range(HALVES):
-            some = slice(half * GAUSS_HALF, (half + 1) * GAUSS_HALF)
-            nc.vector.tensor_tensor(
-                out=f[:, some, :],
-                in0=f_sums[half][:].rearrange("p (q c) -> p q c", c=CHANNELS),
-                in1=b2_all[:, some, :],
-                op=ALU.add,
-            )
-            nc.scalar.activation(out=squares[:, some, :], in_=f[:, some, 7:11], func=ACT.Square)
-            nc.scalar.activation(out=tanhs[:, some, :], in_=f[:, some, 0:7], func=ACT.Tanh, scale=0.5)
+        nc.scalar.activation(out=tanhs[:], in_=f[:, :, 0:7], func=ACT.Tanh, scale=0.5)
+        squares = keep.tile([P, GAUSS, 4], F32)
+        nc.vector.tensor_tensor(out=squares[:], in0=f[:, :, 7:11], in1=f[:, :, 7:11], op=ALU.mult)
+        norm_sq = keep.tile([P, GAUSS], F32)
+        nc.vector.tensor_reduce(
+            out=norm_sq[:], in_=squares[:], axis=mybir.AxisListType.X, op=ALU.add
+        )
+        inv_norm = keep.tile([P, GAUSS], F32)
+        nc.scalar.activation(out=inv_norm[:], in_=norm_sq[:], func=ACT.Abs_reciprocal_sqrt)
         result = keep.tile([P, GAUSS, CHANNELS], F32)
         nc.vector.tensor_scalar(
             out=result[:, :, 11:16],
@@ -257,12 +284,6 @@ def tile_gaussianrenderer_k_kernel(
             op0=ALU.max,
             op1=ALU.min,
         )
-        norm_sq = keep.tile([P, GAUSS], F32)
-        nc.vector.tensor_reduce(
-            out=norm_sq[:], in_=squares[:], axis=mybir.AxisListType.X, op=ALU.add
-        )
-        inv_norm = keep.tile([P, GAUSS], F32)
-        nc.scalar.activation(out=inv_norm[:], in_=norm_sq[:], func=ACT.Abs_reciprocal_sqrt)
         nc.vector.scalar_tensor_tensor(
             out=result[:, :, 0:3],
             in0=tanhs[:, :, 0:3],
@@ -279,12 +300,17 @@ def tile_gaussianrenderer_k_kernel(
             op0=ALU.add,
             op1=ALU.mult,
         )
-        nc.vector.scalar_tensor_tensor(
-            out=result[:, :, 7:11],
-            in0=inv_norm[:].unsqueeze(2).to_broadcast([P, GAUSS, 4]),
-            scalar=1.0e12,
-            in1=f[:, :, 7:11],
-            op0=ALU.min,
-            op1=ALU.mult,
-        )
-        nc.sync.dma_start(out=out_dram, in_=result[:].rearrange("p q c -> p (q c)"))
+        for half in range(HALVES):
+            some = slice(half * GAUSS_HALF, (half + 1) * GAUSS_HALF)
+            nc.vector.scalar_tensor_tensor(
+                out=result[:, some, 7:11],
+                in0=inv_norm[:, some].unsqueeze(2).to_broadcast([P, GAUSS_HALF, 4]),
+                scalar=1.0e12,
+                in1=f[:, some, 7:11],
+                op0=ALU.min,
+                op1=ALU.mult,
+            )
+            nc.sync.dma_start(
+                out=out_dram[:, half * N_PASS : (half + 1) * N_PASS],
+                in_=result[:, some, :].rearrange("p q c -> p (q c)"),
+            )

@@ -33,7 +33,7 @@ EARLY = GROUPS1 - LATE
 W1_BUFS = 20
 SHARED = 4
 SLOTS = GROUPS1 // SHARED
-SYNC_SLOTS = 2
+FIRST_SLOTS = 2
 QUADS = 4
 
 FLOPS = 2 * P * D_IN * WIDTH + 2 * P * WIDTH * WIDTH
@@ -63,9 +63,10 @@ def tile_gaussianrenderer_k_kernel(
         turn = ctx.enter_context(tc.psum_pool(name="turn", bufs=4))
 
         bias_rows = keep.tile([P, 2 * WIDTH], BF16)
-        nc.vector.memset(bias_rows[:], 0.0)
         w1_planes = keep.tile([P, SLOTS, WIDTH], U8, align_bytes=64)
-        nc.vector.memset(w1_planes[:].bitcast(I32), 0)
+        nc.vector.memset(w1_planes[:, 0:FIRST_SLOTS, :].bitcast(I32), 0)
+        nc.vector.memset(w1_planes[:, FIRST_SLOTS:SLOTS, :].bitcast(I32), 0)
+        nc.vector.memset(bias_rows[:], 0.0)
         w2_planes = keep.tile([P, WIDTH], U8, align_bytes=64)
         nc.vector.memset(w2_planes[:].bitcast(I32), 0)
         ones = keep.tile([P, P], BF16)
@@ -91,9 +92,7 @@ def tile_gaussianrenderer_k_kernel(
                     ].bitcast(view),
                 )
 
-        for s in range(SYNC_SLOTS):
-            load_plane_slot(nc.sync, I32, s)
-        for s in range(SYNC_SLOTS, SLOTS):
+        for s in range(SLOTS):
             load_plane_slot(nc.gpsimd, F32, s)
         for quad in range(QUADS):
             nc.gpsimd.dma_start(

@@ -35,6 +35,8 @@ SHARED = 4
 SLOTS = GROUPS1 // SHARED
 FIRST_SLOTS = 2
 QUADS = 4
+PIECES = 2
+PIECE = N_PASS // PIECES
 
 FLOPS = 2 * P * D_IN * WIDTH + 2 * P * WIDTH * WIDTH
 
@@ -73,8 +75,6 @@ def tile_gaussianrenderer_k_kernel(
         nc.vector.memset(ones[:], 1.0)
         ident_f32 = keep.tile([P, P], F32)
         masks.make_identity(nc, ident_f32[:])
-        ident_bf16 = keep.tile([P, P], BF16)
-        masks.make_identity(nc, ident_bf16[:])
 
         x_chunks = []
         chunk_cols = X_CHUNK_GROUPS * K_PASS
@@ -139,7 +139,7 @@ def tile_gaussianrenderer_k_kernel(
                 in_=x_grouped[:],
             )
 
-        b1_all = keep.tile([P, HALVES, PACK, P], F32)
+        b1_all = keep.tile([P, WIDTH], F32)
         b2_all = keep.tile([P, GAUSS, CHANNELS], F32)
         for half in range(HALVES):
             spread = turn.tile([P, N_PASS], F32, tag="turn")
@@ -151,7 +151,7 @@ def tile_gaussianrenderer_k_kernel(
                 stop=True,
             )
             nc.vector.tensor_copy(
-                out=b1_all[:, half, :, :], in_=spread[:].rearrange("p (i t) -> p t i", t=PACK)
+                out=b1_all[:, half * N_PASS : (half + 1) * N_PASS], in_=spread[:]
             )
         for half in range(HALVES):
             spread = turn.tile([P, N_PASS], F32, tag="turn")
@@ -206,39 +206,49 @@ def tile_gaussianrenderer_k_kernel(
 
         h_codes = keep.tile([P, GROUPS2, P], U32, align_bytes=64)
         h_scales = keep.tile([P, GROUPS2, P], U8, align_bytes=64)
-        h_halves = []
-        for half in range(HALVES):
-            for g in range(EARLY, GROUPS1):
-                layer1_pass(g, half)
-            pre = tail.tile([P, PACK, P], F32)
-            nc.vector.tensor_tensor(
-                out=pre[:],
-                in0=h_sums[half][:].rearrange("p (i t) -> p t i", t=PACK),
-                in1=b1_all[:, half, :, :],
-                op=ALU.add,
-            )
-            h_bf16 = tail.tile([P, PACK, P], BF16)
-            nc.scalar.activation(out=h_bf16[:], in_=pre[:], func=ACT.Silu)
-            h_halves.append(h_bf16)
-        h_turned = []
-        for half in range(HALVES):
-            turned = turn.tile([P, PACK, P], BF16, tag="turn")
-            for t in range(PACK):
-                nc.tensor.transpose(turned[:, t, :], h_halves[half][:, t, :], ident_bf16[:])
-            h_turned.append(turned)
-        for half in range(HALVES):
-            h_grouped = tail.tile([P, P, PACK], BF16, align_bytes=64)
-            if half == 0:
-                nc.vector.tensor_copy(
-                    out=h_grouped[:], in_=h_turned[half][:].rearrange("p t r -> p r t")
+
+        def silu_half(half):
+            pre = tail.tile([P, N_PASS], F32)
+            h_bf16 = tail.tile([P, N_PASS], BF16)
+            for piece in range(PIECES):
+                some = slice(piece * PIECE, (piece + 1) * PIECE)
+                nc.vector.tensor_tensor(
+                    out=pre[:, some],
+                    in0=h_sums[half][:, some],
+                    in1=b1_all[:, half * N_PASS + piece * PIECE : half * N_PASS + (piece + 1) * PIECE],
+                    op=ALU.add,
                 )
-            else:
-                nc.scalar.copy(out=h_grouped[:], in_=h_turned[half][:].rearrange("p t r -> p r t"))
+                nc.scalar.activation(out=h_bf16[:, some], in_=pre[:, some], func=ACT.Silu)
+            return h_bf16
+
+        def turn_half(h_bf16):
+            turned = turn.tile([P, 2, P], F32, tag="turn")
+            for u in range(2):
+                nc.tensor.transpose(turned[:, u, :], h_bf16[:].bitcast(F32)[:, u::2], ident_f32[:])
+            h_grouped = tail.tile([P, N_PASS], BF16, align_bytes=64)
+            nc.scalar.copy(
+                out=h_grouped[:].bitcast(F32).rearrange("p (r u) -> p r u", u=2),
+                in_=turned[:].rearrange("p u r -> p r u"),
+            )
+            return h_grouped
+
+        def quantise_half(half, h_grouped):
             nc.vector.quantize_mx(
                 out=h_codes[:, half, :].bitcast(FP8X4),
                 scales=h_scales[:, half, :],
-                in_=h_grouped[:].rearrange("p r t -> p (r t)"),
+                in_=h_grouped[:],
             )
+
+        for g in range(EARLY, GROUPS1):
+            layer1_pass(g, 0)
+        h_first = silu_half(0)
+        for g in range(EARLY, GROUPS1 - 1):
+            layer1_pass(g, 1)
+        h_first_grouped = turn_half(h_first)
+        layer1_pass(GROUPS1 - 1, 1)
+        h_last = silu_half(1)
+        quantise_half(0, h_first_grouped)
+        quantise_half(1, turn_half(h_last))
 
         f_sums = [sums.tile([P, N_PASS], F32, name="f_sum%d" % half) for half in range(HALVES)]
         for g in range(GROUPS2):
@@ -255,7 +265,8 @@ def tile_gaussianrenderer_k_kernel(
                 )
 
         f = keep.tile([P, GAUSS, CHANNELS], F32)
-        for chans in (slice(0, 7), slice(7, CHANNELS)):
+
+        def add_bias(chans):
             for half in range(HALVES):
                 some = slice(half * GAUSS_HALF, (half + 1) * GAUSS_HALF)
                 nc.vector.tensor_tensor(
@@ -264,8 +275,15 @@ def tile_gaussianrenderer_k_kernel(
                     in1=b2_all[:, some, chans],
                     op=ALU.add,
                 )
+
+        add_bias(slice(0, 7))
         tanhs = keep.tile([P, GAUSS, 7], F32)
-        nc.scalar.activation(out=tanhs[:], in_=f[:, :, 0:7], func=ACT.Tanh, scale=0.5)
+        for half in range(HALVES):
+            some = slice(half * GAUSS_HALF, (half + 1) * GAUSS_HALF)
+            nc.scalar.activation(
+                out=tanhs[:, some, :], in_=f[:, some, 0:7], func=ACT.Tanh, scale=0.5
+            )
+        add_bias(slice(7, 11))
         squares = keep.tile([P, GAUSS, 4], F32)
         nc.vector.tensor_tensor(out=squares[:], in0=f[:, :, 7:11], in1=f[:, :, 7:11], op=ALU.mult)
         norm_sq = keep.tile([P, GAUSS], F32)
@@ -274,6 +292,7 @@ def tile_gaussianrenderer_k_kernel(
         )
         inv_norm = keep.tile([P, GAUSS], F32)
         nc.scalar.activation(out=inv_norm[:], in_=norm_sq[:], func=ACT.Abs_reciprocal_sqrt)
+        add_bias(slice(11, CHANNELS))
         result = keep.tile([P, GAUSS, CHANNELS], F32)
         nc.vector.tensor_scalar(
             out=result[:, :, 11:16],

@@ -169,10 +169,6 @@ def tile_gaussianrenderer_k_kernel(
         nc.vector.tensor_scalar_add(out=b2_all[:, :, 11:16], in0=b2_all[:, :, 11:16], scalar1=0.5)
         xyz_shift = keep.tile([P, 3], F32)
         nc.vector.tensor_scalar_add(out=xyz_shift[:], in0=xyz_bf16[:], scalar1=0.1)
-        sig_gain = keep.tile([P, 4], F32)
-        nc.vector.tensor_scalar_mul(out=sig_gain[:, 0:1], in0=ones[:, 0:1], scalar1=0.5)
-        nc.vector.tensor_scalar_mul(out=sig_gain[:, 1:4], in0=ones[:, 1:4], scalar1=0.01)
-
         h_sums = [sums.tile([P, N_PASS], F32, name="h_sum%d" % half) for half in range(HALVES)]
         def layer1_pass(g, half):
             cols = slice(half * N_PASS, (half + 1) * N_PASS)
@@ -264,39 +260,44 @@ def tile_gaussianrenderer_k_kernel(
                     stop=(g == GROUPS2 - 1),
                 )
 
-        f = keep.tile([P, GAUSS, CHANNELS], F32)
+        def dense(chans):
+            return keep.tile([P, GAUSS, chans.stop - chans.start], F32, name="f%d" % chans.start)
 
-        def add_bias(chans):
-            for half in range(HALVES):
-                some = slice(half * GAUSS_HALF, (half + 1) * GAUSS_HALF)
-                nc.vector.tensor_tensor(
-                    out=f[:, some, chans],
-                    in0=f_sums[half][:].rearrange("p (q c) -> p q c", c=CHANNELS)[:, :, chans],
-                    in1=b2_all[:, some, chans],
-                    op=ALU.add,
-                )
+        def add_bias(summed, chans, half):
+            some = slice(half * GAUSS_HALF, (half + 1) * GAUSS_HALF)
+            nc.vector.tensor_tensor(
+                out=summed[:, some, :],
+                in0=f_sums[half][:].rearrange("p (q c) -> p q c", c=CHANNELS)[:, :, chans],
+                in1=b2_all[:, some, chans],
+                op=ALU.add,
+            )
 
-        add_bias(slice(0, 7))
+        sigmoid_chans, rot_chans, rgb_chans = slice(0, 7), slice(7, 11), slice(11, CHANNELS)
+        f_sigmoid, f_rot, f_rgb = dense(sigmoid_chans), dense(rot_chans), dense(rgb_chans)
+        for half in range(HALVES):
+            add_bias(f_sigmoid, sigmoid_chans, half)
         tanhs = keep.tile([P, GAUSS, 7], F32)
         for half in range(HALVES):
             some = slice(half * GAUSS_HALF, (half + 1) * GAUSS_HALF)
             nc.scalar.activation(
-                out=tanhs[:, some, :], in_=f[:, some, 0:7], func=ACT.Tanh, scale=0.5
+                out=tanhs[:, some, :], in_=f_sigmoid[:, some, :], func=ACT.Tanh, scale=0.5
             )
-        add_bias(slice(7, 11))
+        for half in range(HALVES):
+            add_bias(f_rot, rot_chans, half)
+        add_bias(f_rgb, rgb_chans, 0)
         squares = keep.tile([P, GAUSS, 4], F32)
-        nc.vector.tensor_tensor(out=squares[:], in0=f[:, :, 7:11], in1=f[:, :, 7:11], op=ALU.mult)
+        nc.vector.tensor_tensor(out=squares[:], in0=f_rot[:], in1=f_rot[:], op=ALU.mult)
+        add_bias(f_rgb, rgb_chans, 1)
         norm_sq = keep.tile([P, GAUSS], F32)
         nc.vector.tensor_reduce(
             out=norm_sq[:], in_=squares[:], axis=mybir.AxisListType.X, op=ALU.add
         )
         inv_norm = keep.tile([P, GAUSS], F32)
         nc.scalar.activation(out=inv_norm[:], in_=norm_sq[:], func=ACT.Abs_reciprocal_sqrt)
-        add_bias(slice(11, CHANNELS))
         result = keep.tile([P, GAUSS, CHANNELS], F32)
         nc.vector.tensor_scalar(
             out=result[:, :, 11:16],
-            in0=f[:, :, 11:16],
+            in0=f_rgb[:],
             scalar1=0.0,
             scalar2=1.0,
             op0=ALU.max,
@@ -310,21 +311,19 @@ def tile_gaussianrenderer_k_kernel(
             op0=ALU.mult,
             op1=ALU.add,
         )
-        nc.vector.scalar_tensor_tensor(
-            out=result[:, :, 3:7],
-            in0=tanhs[:, :, 3:7],
-            scalar=1.0,
-            in1=sig_gain[:].unsqueeze(1).to_broadcast([P, GAUSS, 4]),
-            op0=ALU.add,
-            op1=ALU.mult,
-        )
         for half in range(HALVES):
             some = slice(half * GAUSS_HALF, (half + 1) * GAUSS_HALF)
+            nc.scalar.activation(
+                out=result[:, some, 3:4], in_=tanhs[:, some, 3:4], func=ACT.Copy, scale=0.5, bias=0.5
+            )
+            nc.scalar.activation(
+                out=result[:, some, 4:7], in_=tanhs[:, some, 4:7], func=ACT.Copy, scale=0.01, bias=0.01
+            )
             nc.vector.scalar_tensor_tensor(
                 out=result[:, some, 7:11],
                 in0=inv_norm[:, some].unsqueeze(2).to_broadcast([P, GAUSS_HALF, 4]),
                 scalar=1.0e12,
-                in1=f[:, some, 7:11],
+                in1=f_rot[:, some, :],
                 op0=ALU.min,
                 op1=ALU.mult,
             )

@@ -34,7 +34,10 @@ W1_BUFS = 20
 SHARED = 4
 SLOTS = GROUPS1 // SHARED
 FIRST_SLOTS = 2
+GPSIMD_SLOTS = 6
+FIRST_SMALL = 6
 QUADS = 4
+DUMMIES = 2
 PIECES = 2
 PIECE = N_PASS // PIECES
 
@@ -50,7 +53,7 @@ def tile_gaussianrenderer_k_kernel(
     xyz_dram = xyzs.rearrange("b n c -> (b n) c")
     w1_dram = W1_words.rearrange("g p n t -> p g (n t)").bitcast(I32)
     w2_dram = W2_words.rearrange("g p n t -> p g (n t)").bitcast(I32)
-    w2_scale_dram = W2_scales.bitcast(F32)
+    w2_scale_dram = W2_scales.bitcast(I32)
     out_dram = out.rearrange("b (n q) c -> (b n) (q c)", q=GAUSS)
 
     with ExitStack() as ctx:
@@ -64,15 +67,14 @@ def tile_gaussianrenderer_k_kernel(
         sums = ctx.enter_context(tc.psum_pool(name="sums", bufs=1))
         turn = ctx.enter_context(tc.psum_pool(name="turn", bufs=4))
 
-        bias_rows = keep.tile([P, 2 * WIDTH], BF16)
+        ones = keep.tile([P, P], BF16)
+        nc.vector.memset(ones[:], 1.0)
         w1_planes = keep.tile([P, SLOTS, WIDTH], U8, align_bytes=64)
         nc.vector.memset(w1_planes[:, 0:FIRST_SLOTS, :].bitcast(I32), 0)
         nc.vector.memset(w1_planes[:, FIRST_SLOTS:SLOTS, :].bitcast(I32), 0)
-        nc.vector.memset(bias_rows[:], 0.0)
         w2_planes = keep.tile([P, WIDTH], U8, align_bytes=64)
         nc.vector.memset(w2_planes[:].bitcast(I32), 0)
-        ones = keep.tile([P, P], BF16)
-        nc.vector.memset(ones[:], 1.0)
+        bias_rows = keep.tile([P, 2 * WIDTH], BF16)
         ident_f32 = keep.tile([P, P], F32)
         masks.make_identity(nc, ident_f32[:])
 
@@ -83,34 +85,33 @@ def tile_gaussianrenderer_k_kernel(
             nc.sync.dma_start(out=x_sb[:], in_=x_dram[:, c * chunk_cols : (c + 1) * chunk_cols])
             x_chunks.append(x_sb)
 
-        def load_plane_slot(queue, view, s):
-            for quad in range(QUADS):
-                queue.dma_start(
-                    out=w1_planes[32 * quad : 32 * quad + 4 * SHARED, s, :].bitcast(view),
-                    in_=W1_scales[
-                        SHARED * s : SHARED * (s + 1), 4 * quad : 4 * quad + 4, :
-                    ].bitcast(view),
-                )
-
-        for s in range(SLOTS):
-            load_plane_slot(nc.gpsimd, F32, s)
-        for quad in range(QUADS):
-            nc.gpsimd.dma_start(
-                out=w2_planes[32 * quad : 32 * quad + 4 * GROUPS2, :].bitcast(F32),
-                in_=w2_scale_dram[:, 4 * quad : 4 * quad + 4, :],
+        def load_plane_quad(queue, view, s, quad):
+            queue.dma_start(
+                out=w1_planes[32 * quad : 32 * quad + 4 * SHARED, s, :].bitcast(view),
+                in_=W1_scales[SHARED * s : SHARED * (s + 1), 4 * quad : 4 * quad + 4, :].bitcast(view),
             )
+
+        for s in range(GPSIMD_SLOTS):
+            for quad in range(QUADS):
+                load_plane_quad(nc.gpsimd, F32, s, quad)
 
         def load_w1(g):
             w1_sb = w1_pool.tile([P, WIDTH], U32, align_bytes=64)
             nc.sync.dma_start(out=w1_sb[:].bitcast(I32), in_=w1_dram[:, g, :])
             return w1_sb
 
-        w1_tiles = [load_w1(g) for g in range(W1_BUFS)]
+        w1_tiles = []
+        for g in range(W1_BUFS):
+            w1_tiles.append(load_w1(g))
+            s, quad = divmod(g - FIRST_SMALL, QUADS)
+            if 0 <= s < SLOTS - GPSIMD_SLOTS:
+                load_plane_quad(nc.sync, I32, GPSIMD_SLOTS + s, quad)
+            elif s == SLOTS - GPSIMD_SLOTS:
+                nc.sync.dma_start(
+                    out=w2_planes[32 * quad : 32 * quad + 4 * GROUPS2, :].bitcast(I32),
+                    in_=w2_scale_dram[:, 4 * quad : 4 * quad + 4, :],
+                )
 
-        nc.scalar.dma_start(out=bias_rows[0:1, 0:WIDTH], in_=b1.unsqueeze(0))
-        nc.scalar.dma_start(out=bias_rows[0:1, WIDTH : 2 * WIDTH], in_=b2.unsqueeze(0))
-        xyz_bf16 = keep.tile([P, 3], BF16)
-        nc.scalar.dma_start(out=xyz_bf16[:], in_=xyz_dram)
         warm = keep.tile([P, 1], F32)
         nc.scalar.activation(out=warm[:], in_=ones[:, 0:1], func=ACT.Silu)
 
@@ -138,6 +139,43 @@ def tile_gaussianrenderer_k_kernel(
                 scales=x_scales[:, g0 : g0 + BANK_GROUPS, :].rearrange("p g r -> p (g r)"),
                 in_=x_grouped[:],
             )
+
+        nc.vector.memset(bias_rows[:], 0.0)
+        nc.scalar.dma_start(out=bias_rows[0:1, 0:WIDTH], in_=b1.unsqueeze(0))
+        nc.scalar.dma_start(out=bias_rows[0:1, WIDTH : 2 * WIDTH], in_=b2.unsqueeze(0))
+        xyz_bf16 = keep.tile([P, 3], BF16)
+        nc.scalar.dma_start(out=xyz_bf16[:], in_=xyz_dram)
+
+        h_sums = [sums.tile([P, N_PASS], F32, name="h_sum%d" % half) for half in range(HALVES)]
+        def layer1_pass(g, half):
+            cols = slice(half * N_PASS, (half + 1) * N_PASS)
+            nc.tensor.matmul_mx(
+                out=h_sums[half][:],
+                lhsT=x_codes[:, g, :].bitcast(FP8X4),
+                lhsT_scale=x_scales[:, g, :],
+                rhs=w1_tiles[g][:, cols].bitcast(FP8X4),
+                rhs_scale=w1_planes[4 * (g % SHARED) : P, g // SHARED, cols],
+                start=(g == 0),
+                stop=(g == GROUPS1 - 1),
+            )
+
+        for g in range(EARLY - W1_BUFS):
+            for half in range(HALVES):
+                layer1_pass(g, half)
+            w1_tiles.append(load_w1(g + W1_BUFS))
+        for g in range(EARLY, GROUPS1):
+            w1_late = late_pool.tile([P, WIDTH], U32, align_bytes=64)
+            w1_tiles.append(w1_late)
+        for half in range(HALVES):
+            cols = slice(half * N_PASS, (half + 1) * N_PASS)
+            for g in range(EARLY, GROUPS1):
+                nc.sync.dma_start(out=w1_tiles[g][:, cols].bitcast(I32), in_=w1_dram[:, g, cols])
+        w2_words = keep.tile([P, GROUPS2, WIDTH], U32, align_bytes=64)
+        for g in range(GROUPS2):
+            nc.sync.dma_start(out=w2_words[:, g, :].bitcast(I32), in_=w2_dram[:, g, :])
+        for g in range(EARLY - W1_BUFS, W1_BUFS):
+            for half in range(HALVES):
+                layer1_pass(g, half)
 
         b1_all = keep.tile([P, WIDTH], F32)
         b2_all = keep.tile([P, GAUSS, CHANNELS], F32)
@@ -169,34 +207,8 @@ def tile_gaussianrenderer_k_kernel(
         nc.vector.tensor_scalar_add(out=b2_all[:, :, 11:16], in0=b2_all[:, :, 11:16], scalar1=0.5)
         xyz_shift = keep.tile([P, 3], F32)
         nc.vector.tensor_scalar_add(out=xyz_shift[:], in0=xyz_bf16[:], scalar1=0.1)
-        h_sums = [sums.tile([P, N_PASS], F32, name="h_sum%d" % half) for half in range(HALVES)]
-        def layer1_pass(g, half):
-            cols = slice(half * N_PASS, (half + 1) * N_PASS)
-            nc.tensor.matmul_mx(
-                out=h_sums[half][:],
-                lhsT=x_codes[:, g, :].bitcast(FP8X4),
-                lhsT_scale=x_scales[:, g, :],
-                rhs=w1_tiles[g][:, cols].bitcast(FP8X4),
-                rhs_scale=w1_planes[4 * (g % SHARED) : P, g // SHARED, cols],
-                start=(g == 0),
-                stop=(g == GROUPS1 - 1),
-            )
 
-        for g in range(EARLY - W1_BUFS):
-            for half in range(HALVES):
-                layer1_pass(g, half)
-            w1_tiles.append(load_w1(g + W1_BUFS))
-        for g in range(EARLY, GROUPS1):
-            w1_late = late_pool.tile([P, WIDTH], U32, align_bytes=64)
-            w1_tiles.append(w1_late)
-        for half in range(HALVES):
-            cols = slice(half * N_PASS, (half + 1) * N_PASS)
-            for g in range(EARLY, GROUPS1):
-                nc.sync.dma_start(out=w1_tiles[g][:, cols].bitcast(I32), in_=w1_dram[:, g, cols])
-        w2_words = keep.tile([P, GROUPS2, WIDTH], U32, align_bytes=64)
-        for g in range(GROUPS2):
-            nc.sync.dma_start(out=w2_words[:, g, :].bitcast(I32), in_=w2_dram[:, g, :])
-        for g in range(EARLY - W1_BUFS, EARLY):
+        for g in range(W1_BUFS, EARLY):
             for half in range(HALVES):
                 layer1_pass(g, half)
 
@@ -221,8 +233,12 @@ def tile_gaussianrenderer_k_kernel(
             turned = turn.tile([P, 2, P], F32, tag="turn")
             for u in range(2):
                 nc.tensor.transpose(turned[:, u, :], h_bf16[:].bitcast(F32)[:, u::2], ident_f32[:])
+            return turned
+
+        def group_half(half, turned):
             h_grouped = tail.tile([P, N_PASS], BF16, align_bytes=64)
-            nc.scalar.copy(
+            copy = nc.vector.tensor_copy if half == 0 else nc.scalar.copy
+            copy(
                 out=h_grouped[:].bitcast(F32).rearrange("p (r u) -> p r u", u=2),
                 in_=turned[:].rearrange("p u r -> p r u"),
             )
@@ -235,16 +251,19 @@ def tile_gaussianrenderer_k_kernel(
                 in_=h_grouped[:],
             )
 
-        for g in range(EARLY, GROUPS1):
-            layer1_pass(g, 0)
-        h_first = silu_half(0)
-        for g in range(EARLY, GROUPS1 - 1):
-            layer1_pass(g, 1)
-        h_first_grouped = turn_half(h_first)
-        layer1_pass(GROUPS1 - 1, 1)
-        h_last = silu_half(1)
-        quantise_half(0, h_first_grouped)
-        quantise_half(1, turn_half(h_last))
+        h_halves = []
+        for half in range(HALVES):
+            for g in range(EARLY, GROUPS1):
+                layer1_pass(g, half)
+            h_halves.append(silu_half(half))
+        turned = turn_half(h_halves[0])
+        for dummy in range(DUMMIES):
+            idle = turn.tile([P, N_PASS], F32, tag="turn")
+            nc.tensor.matmul(
+                out=idle[:], lhsT=ones[:], rhs=bias_rows[:, 0:N_PASS], start=True, stop=True
+            )
+        quantise_half(0, group_half(0, turned))
+        quantise_half(1, group_half(1, turn_half(h_halves[1])))
 
         f_sums = [sums.tile([P, N_PASS], F32, name="f_sum%d" % half) for half in range(HALVES)]
         for g in range(GROUPS2):

@@ -30,12 +30,12 @@ X_CHUNK_GROUPS = GROUPS1 // X_CHUNKS
 BANK_GROUPS = 2
 LATE = 4
 EARLY = GROUPS1 - LATE
-W1_BUFS = 20
+PAIR = 2
+PAIRS = EARLY // PAIR
+W1_BUFS = 10
 SHARED = 4
 SLOTS = GROUPS1 // SHARED
 FIRST_SLOTS = 2
-GPSIMD_SLOTS = 6
-FIRST_SMALL = 6
 QUADS = 4
 DUMMIES = 2
 PIECES = 2
@@ -61,7 +61,6 @@ def tile_gaussianrenderer_k_kernel(
         keep = ctx.enter_context(tc.tile_pool(name="keep", bufs=1))
         x_pool = ctx.enter_context(tc.tile_pool(name="x", bufs=X_CHUNKS))
         w1_pool = ctx.enter_context(tc.tile_pool(name="w1", bufs=W1_BUFS))
-        late_pool = ctx.enter_context(tc.tile_pool(name="late", bufs=LATE))
         stage = ctx.enter_context(tc.tile_pool(name="stage", bufs=4))
         tail = ctx.enter_context(tc.tile_pool(name="tail", bufs=2))
         sums = ctx.enter_context(tc.psum_pool(name="sums", bufs=1))
@@ -78,39 +77,48 @@ def tile_gaussianrenderer_k_kernel(
         ident_f32 = keep.tile([P, P], F32)
         masks.make_identity(nc, ident_f32[:])
 
-        x_chunks = []
-        chunk_cols = X_CHUNK_GROUPS * K_PASS
-        for c in range(X_CHUNKS):
-            x_sb = x_pool.tile([P, chunk_cols], BF16)
-            nc.sync.dma_start(out=x_sb[:], in_=x_dram[:, c * chunk_cols : (c + 1) * chunk_cols])
-            x_chunks.append(x_sb)
-
         def load_plane_quad(queue, view, s, quad):
             queue.dma_start(
                 out=w1_planes[32 * quad : 32 * quad + 4 * SHARED, s, :].bitcast(view),
                 in_=W1_scales[SHARED * s : SHARED * (s + 1), 4 * quad : 4 * quad + 4, :].bitcast(view),
             )
 
-        for s in range(GPSIMD_SLOTS):
-            for quad in range(QUADS):
+        def load_w2_plane_quad(quad):
+            nc.sync.dma_start(
+                out=w2_planes[32 * quad : 32 * quad + 4 * GROUPS2, :].bitcast(I32),
+                in_=w2_scale_dram[:, 4 * quad : 4 * quad + 4, :],
+            )
+
+        small_loads = [
+            lambda s=s, quad=quad: load_plane_quad(nc.sync, I32, s, quad)
+            for s in range(SLOTS)
+            for quad in (0, 1)
+        ]
+        small_loads.extend([lambda quad=quad: load_w2_plane_quad(quad) for quad in range(QUADS)])
+        for s in range(SLOTS):
+            for quad in (2, 3):
                 load_plane_quad(nc.gpsimd, F32, s, quad)
 
-        def load_w1(g):
-            w1_sb = w1_pool.tile([P, WIDTH], U32, align_bytes=64)
-            nc.sync.dma_start(out=w1_sb[:].bitcast(I32), in_=w1_dram[:, g, :])
-            return w1_sb
+        x_chunks = []
+        chunk_cols = X_CHUNK_GROUPS * K_PASS
+        for c in range(X_CHUNKS):
+            x_sb = x_pool.tile([P, chunk_cols], BF16)
+            nc.sync.dma_start(out=x_sb[:], in_=x_dram[:, c * chunk_cols : (c + 1) * chunk_cols])
+            x_chunks.append(x_sb)
+            small_loads[c]()
 
-        w1_tiles = []
-        for g in range(W1_BUFS):
-            w1_tiles.append(load_w1(g))
-            s, quad = divmod(g - FIRST_SMALL, QUADS)
-            if 0 <= s < SLOTS - GPSIMD_SLOTS:
-                load_plane_quad(nc.sync, I32, GPSIMD_SLOTS + s, quad)
-            elif s == SLOTS - GPSIMD_SLOTS:
-                nc.sync.dma_start(
-                    out=w2_planes[32 * quad : 32 * quad + 4 * GROUPS2, :].bitcast(I32),
-                    in_=w2_scale_dram[:, 4 * quad : 4 * quad + 4, :],
-                )
+        w1_pairs = []
+
+        def load_w1_pair():
+            w1_sb = w1_pool.tile([P, PAIR, WIDTH], U32, align_bytes=64)
+            g0 = PAIR * len(w1_pairs)
+            nc.sync.dma_start(out=w1_sb[:].bitcast(I32), in_=w1_dram[:, g0 : g0 + PAIR, :])
+            w1_pairs.append(w1_sb)
+
+        for n in range(W1_BUFS):
+            load_w1_pair()
+            for small in small_loads[X_CHUNKS + PAIR * n : X_CHUNKS + PAIR * (n + 1)]:
+                small()
 
         warm = keep.tile([P, 1], F32)
         nc.scalar.activation(out=warm[:], in_=ones[:, 0:1], func=ACT.Silu)
@@ -147,35 +155,42 @@ def tile_gaussianrenderer_k_kernel(
         nc.scalar.dma_start(out=xyz_bf16[:], in_=xyz_dram)
 
         h_sums = [sums.tile([P, N_PASS], F32, name="h_sum%d" % half) for half in range(HALVES)]
+
+        def w1_columns(g, cols):
+            if g < EARLY:
+                return w1_pairs[g // PAIR][:, g % PAIR, cols]
+            return w1_late[:, g - EARLY, cols]
+
         def layer1_pass(g, half):
             cols = slice(half * N_PASS, (half + 1) * N_PASS)
             nc.tensor.matmul_mx(
                 out=h_sums[half][:],
                 lhsT=x_codes[:, g, :].bitcast(FP8X4),
                 lhsT_scale=x_scales[:, g, :],
-                rhs=w1_tiles[g][:, cols].bitcast(FP8X4),
+                rhs=w1_columns(g, cols).bitcast(FP8X4),
                 rhs_scale=w1_planes[4 * (g % SHARED) : P, g // SHARED, cols],
                 start=(g == 0),
                 stop=(g == GROUPS1 - 1),
             )
 
-        for g in range(EARLY - W1_BUFS):
-            for half in range(HALVES):
-                layer1_pass(g, half)
-            w1_tiles.append(load_w1(g + W1_BUFS))
-        for g in range(EARLY, GROUPS1):
-            w1_late = late_pool.tile([P, WIDTH], U32, align_bytes=64)
-            w1_tiles.append(w1_late)
-        for half in range(HALVES):
+        def layer1_groups(groups):
+            for g in groups:
+                for half in range(HALVES):
+                    layer1_pass(g, half)
+
+        for n in range(PAIRS - W1_BUFS):
+            layer1_groups(range(PAIR * n, PAIR * (n + 1)))
+            load_w1_pair()
+        w1_late = keep.tile([P, LATE, WIDTH], U32, align_bytes=64)
+        for g0, g1, half in ((EARLY, GROUPS1, 0), (EARLY, GROUPS1 - 1, 1), (GROUPS1 - 1, GROUPS1, 1)):
             cols = slice(half * N_PASS, (half + 1) * N_PASS)
-            for g in range(EARLY, GROUPS1):
-                nc.sync.dma_start(out=w1_tiles[g][:, cols].bitcast(I32), in_=w1_dram[:, g, cols])
+            nc.sync.dma_start(
+                out=w1_late[:, g0 - EARLY : g1 - EARLY, cols].bitcast(I32), in_=w1_dram[:, g0:g1, cols]
+            )
         w2_words = keep.tile([P, GROUPS2, WIDTH], U32, align_bytes=64)
         for g in range(GROUPS2):
             nc.sync.dma_start(out=w2_words[:, g, :].bitcast(I32), in_=w2_dram[:, g, :])
-        for g in range(EARLY - W1_BUFS, W1_BUFS):
-            for half in range(HALVES):
-                layer1_pass(g, half)
+        layer1_groups(range(PAIR * (PAIRS - W1_BUFS), PAIR * W1_BUFS))
 
         b1_all = keep.tile([P, WIDTH], F32)
         b2_all = keep.tile([P, GAUSS, CHANNELS], F32)
@@ -208,9 +223,7 @@ def tile_gaussianrenderer_k_kernel(
         xyz_shift = keep.tile([P, 3], F32)
         nc.vector.tensor_scalar_add(out=xyz_shift[:], in0=xyz_bf16[:], scalar1=0.1)
 
-        for g in range(W1_BUFS, EARLY):
-            for half in range(HALVES):
-                layer1_pass(g, half)
+        layer1_groups(range(PAIR * W1_BUFS, EARLY))
 
         h_codes = keep.tile([P, GROUPS2, P], U32, align_bytes=64)
         h_scales = keep.tile([P, GROUPS2, P], U8, align_bytes=64)

@@ -24,19 +24,20 @@ GROUPS2 = WIDTH // K_PASS
 CHANNELS = 16
 GAUSS = WIDTH // CHANNELS
 GAUSS_HALF = GAUSS // HALVES
+GAUSS_FIRST = 48
 
 X_CHUNKS = 4
 X_CHUNK_GROUPS = GROUPS1 // X_CHUNKS
 BANK_GROUPS = 2
-LATE = 4
+LATE = 2
 EARLY = GROUPS1 - LATE
 PAIR = 2
 PAIRS = EARLY // PAIR
-W1_BUFS = 10
+W1_BUFS = 13
 SHARED = 4
 SLOTS = GROUPS1 // SHARED
-FIRST_SLOTS = 2
 QUADS = 4
+PLANE_ROWS = 4
 DUMMIES = 2
 PIECES = 2
 PIECE = N_PASS // PIECES
@@ -69,35 +70,21 @@ def tile_gaussianrenderer_k_kernel(
         ones = keep.tile([P, P], BF16)
         nc.vector.memset(ones[:], 1.0)
         w1_planes = keep.tile([P, SLOTS, WIDTH], U8, align_bytes=64)
-        nc.vector.memset(w1_planes[:, 0:FIRST_SLOTS, :].bitcast(I32), 0)
-        nc.vector.memset(w1_planes[:, FIRST_SLOTS:SLOTS, :].bitcast(I32), 0)
+        nc.vector.memset(w1_planes[:].bitcast(I32), 0)
         w2_planes = keep.tile([P, WIDTH], U8, align_bytes=64)
         nc.vector.memset(w2_planes[:].bitcast(I32), 0)
         bias_rows = keep.tile([P, 2 * WIDTH], BF16)
         ident_f32 = keep.tile([P, P], F32)
         masks.make_identity(nc, ident_f32[:])
 
-        def load_plane_quad(queue, view, s, quad):
-            queue.dma_start(
-                out=w1_planes[32 * quad : 32 * quad + 4 * SHARED, s, :].bitcast(view),
-                in_=W1_scales[SHARED * s : SHARED * (s + 1), 4 * quad : 4 * quad + 4, :].bitcast(view),
-            )
-
-        def load_w2_plane_quad(quad):
-            nc.sync.dma_start(
-                out=w2_planes[32 * quad : 32 * quad + 4 * GROUPS2, :].bitcast(I32),
-                in_=w2_scale_dram[:, 4 * quad : 4 * quad + 4, :],
-            )
-
-        small_loads = [
-            lambda s=s, quad=quad: load_plane_quad(nc.sync, I32, s, quad)
-            for s in range(SLOTS)
-            for quad in (0, 1)
-        ]
-        small_loads.extend([lambda quad=quad: load_w2_plane_quad(quad) for quad in range(QUADS)])
-        for s in range(SLOTS):
-            for quad in (2, 3):
-                load_plane_quad(nc.gpsimd, F32, s, quad)
+        for r in range(PLANE_ROWS):
+            for quad in range(QUADS):
+                nc.gpsimd.dma_start(
+                    out=w1_planes[32 * quad + r : 32 * quad + 4 * SHARED : 4, :, :].bitcast(F32),
+                    in_=W1_scales[:, 4 * quad + r, :]
+                    .rearrange("(s j) n -> j s n", j=SHARED)
+                    .bitcast(F32),
+                )
 
         x_chunks = []
         chunk_cols = X_CHUNK_GROUPS * K_PASS
@@ -105,7 +92,6 @@ def tile_gaussianrenderer_k_kernel(
             x_sb = x_pool.tile([P, chunk_cols], BF16)
             nc.sync.dma_start(out=x_sb[:], in_=x_dram[:, c * chunk_cols : (c + 1) * chunk_cols])
             x_chunks.append(x_sb)
-            small_loads[c]()
 
         w1_pairs = []
 
@@ -117,8 +103,12 @@ def tile_gaussianrenderer_k_kernel(
 
         for n in range(W1_BUFS):
             load_w1_pair()
-            for small in small_loads[X_CHUNKS + PAIR * n : X_CHUNKS + PAIR * (n + 1)]:
-                small()
+            if 1 <= n <= QUADS:
+                quad = n - 1
+                nc.sync.dma_start(
+                    out=w2_planes[32 * quad : 32 * quad + 4 * GROUPS2, :].bitcast(I32),
+                    in_=w2_scale_dram[:, 4 * quad : 4 * quad + 4, :],
+                )
 
         warm = keep.tile([P, 1], F32)
         nc.scalar.activation(out=warm[:], in_=ones[:, 0:1], func=ACT.Silu)
@@ -230,7 +220,7 @@ def tile_gaussianrenderer_k_kernel(
 
         def silu_half(half):
             pre = tail.tile([P, N_PASS], F32)
-            h_bf16 = tail.tile([P, N_PASS], BF16)
+            h_bf16 = tail.tile([P, 2, P, 2], BF16)
             for piece in range(PIECES):
                 some = slice(piece * PIECE, (piece + 1) * PIECE)
                 nc.vector.tensor_tensor(
@@ -239,13 +229,21 @@ def tile_gaussianrenderer_k_kernel(
                     in1=b1_all[:, half * N_PASS + piece * PIECE : half * N_PASS + (piece + 1) * PIECE],
                     op=ALU.add,
                 )
-                nc.scalar.activation(out=h_bf16[:, some], in_=pre[:, some], func=ACT.Silu)
+                nc.scalar.activation(
+                    out=h_bf16[:, :, piece * P // PIECES : (piece + 1) * P // PIECES, :],
+                    in_=pre[:, some].rearrange("p (i u e) -> p u i e", u=2, e=2),
+                    func=ACT.Silu,
+                )
             return h_bf16
 
         def turn_half(h_bf16):
             turned = turn.tile([P, 2, P], F32, tag="turn")
             for u in range(2):
-                nc.tensor.transpose(turned[:, u, :], h_bf16[:].bitcast(F32)[:, u::2], ident_f32[:])
+                nc.tensor.transpose(
+                    turned[:, u, :],
+                    h_bf16[:, u, :, :].rearrange("p i e -> p (i e)").bitcast(F32),
+                    ident_f32[:],
+                )
             return turned
 
         def group_half(half, turned):
@@ -343,8 +341,8 @@ def tile_gaussianrenderer_k_kernel(
             op0=ALU.mult,
             op1=ALU.add,
         )
-        for half in range(HALVES):
-            some = slice(half * GAUSS_HALF, (half + 1) * GAUSS_HALF)
+        for q0, q1 in ((0, GAUSS_FIRST), (GAUSS_FIRST, GAUSS)):
+            some = slice(q0, q1)
             nc.scalar.activation(
                 out=result[:, some, 3:4], in_=tanhs[:, some, 3:4], func=ACT.Copy, scale=0.5, bias=0.5
             )
@@ -353,13 +351,13 @@ def tile_gaussianrenderer_k_kernel(
             )
             nc.vector.scalar_tensor_tensor(
                 out=result[:, some, 7:11],
-                in0=inv_norm[:, some].unsqueeze(2).to_broadcast([P, GAUSS_HALF, 4]),
+                in0=inv_norm[:, some].unsqueeze(2).to_broadcast([P, q1 - q0, 4]),
                 scalar=1.0e12,
                 in1=f_rot[:, some, :],
                 op0=ALU.min,
                 op1=ALU.mult,
             )
             nc.sync.dma_start(
-                out=out_dram[:, half * N_PASS : (half + 1) * N_PASS],
+                out=out_dram[:, q0 * CHANNELS : q1 * CHANNELS],
                 in_=result[:, some, :].rearrange("p q c -> p (q c)"),
             )

@@ -36,10 +36,11 @@ PAIRS = EARLY // PAIR
 W1_BUFS = 13
 SHARED = 4
 SLOTS = GROUPS1 // SHARED
+DMA_ALIGN = 256
 QUADS = 4
 PLANE_ROWS = 4
 DUMMIES = 2
-PIECES = 2
+PIECES = 4
 PIECE = N_PASS // PIECES
 
 FLOPS = 2 * P * D_IN * WIDTH + 2 * P * WIDTH * WIDTH
@@ -54,7 +55,7 @@ def tile_gaussianrenderer_k_kernel(
     xyz_dram = xyzs.rearrange("b n c -> (b n) c")
     w1_dram = W1_words.rearrange("g p n t -> p g (n t)").bitcast(I32)
     w2_dram = W2_words.rearrange("g p n t -> p g (n t)").bitcast(I32)
-    w2_scale_dram = W2_scales.bitcast(I32)
+    w2_scale_dram = W2_scales.bitcast(F32)
     out_dram = out.rearrange("b (n q) c -> (b n) (q c)", q=GAUSS)
 
     with ExitStack() as ctx:
@@ -69,9 +70,9 @@ def tile_gaussianrenderer_k_kernel(
 
         ones = keep.tile([P, P], BF16)
         nc.vector.memset(ones[:], 1.0)
-        w1_planes = keep.tile([P, SLOTS, WIDTH], U8, align_bytes=64)
+        w1_planes = keep.tile([P, SLOTS, WIDTH], U8, align_bytes=DMA_ALIGN)
         nc.vector.memset(w1_planes[:].bitcast(I32), 0)
-        w2_planes = keep.tile([P, WIDTH], U8, align_bytes=64)
+        w2_planes = keep.tile([P, WIDTH], U8, align_bytes=DMA_ALIGN)
         nc.vector.memset(w2_planes[:].bitcast(I32), 0)
         bias_rows = keep.tile([P, 2 * WIDTH], BF16)
         ident_f32 = keep.tile([P, P], F32)
@@ -86,29 +87,29 @@ def tile_gaussianrenderer_k_kernel(
                     .bitcast(F32),
                 )
 
+        for quad in range(QUADS):
+            nc.gpsimd.dma_start(
+                out=w2_planes[32 * quad : 32 * quad + 4 * GROUPS2, :].bitcast(F32),
+                in_=w2_scale_dram[:, 4 * quad : 4 * quad + 4, :],
+            )
+
         x_chunks = []
         chunk_cols = X_CHUNK_GROUPS * K_PASS
         for c in range(X_CHUNKS):
-            x_sb = x_pool.tile([P, chunk_cols], BF16)
+            x_sb = x_pool.tile([P, chunk_cols], BF16, align_bytes=DMA_ALIGN)
             nc.sync.dma_start(out=x_sb[:], in_=x_dram[:, c * chunk_cols : (c + 1) * chunk_cols])
             x_chunks.append(x_sb)
 
         w1_pairs = []
 
         def load_w1_pair():
-            w1_sb = w1_pool.tile([P, PAIR, WIDTH], U32, align_bytes=64)
+            w1_sb = w1_pool.tile([P, PAIR, WIDTH], U32, align_bytes=DMA_ALIGN)
             g0 = PAIR * len(w1_pairs)
             nc.sync.dma_start(out=w1_sb[:].bitcast(I32), in_=w1_dram[:, g0 : g0 + PAIR, :])
             w1_pairs.append(w1_sb)
 
         for n in range(W1_BUFS):
             load_w1_pair()
-            if 1 <= n <= QUADS:
-                quad = n - 1
-                nc.sync.dma_start(
-                    out=w2_planes[32 * quad : 32 * quad + 4 * GROUPS2, :].bitcast(I32),
-                    in_=w2_scale_dram[:, 4 * quad : 4 * quad + 4, :],
-                )
 
         warm = keep.tile([P, 1], F32)
         nc.scalar.activation(out=warm[:], in_=ones[:, 0:1], func=ACT.Silu)
@@ -171,13 +172,13 @@ def tile_gaussianrenderer_k_kernel(
         for n in range(PAIRS - W1_BUFS):
             layer1_groups(range(PAIR * n, PAIR * (n + 1)))
             load_w1_pair()
-        w1_late = keep.tile([P, LATE, WIDTH], U32, align_bytes=64)
+        w1_late = keep.tile([P, LATE, WIDTH], U32, align_bytes=DMA_ALIGN)
         for g0, g1, half in ((EARLY, GROUPS1, 0), (EARLY, GROUPS1 - 1, 1), (GROUPS1 - 1, GROUPS1, 1)):
             cols = slice(half * N_PASS, (half + 1) * N_PASS)
             nc.sync.dma_start(
                 out=w1_late[:, g0 - EARLY : g1 - EARLY, cols].bitcast(I32), in_=w1_dram[:, g0:g1, cols]
             )
-        w2_words = keep.tile([P, GROUPS2, WIDTH], U32, align_bytes=64)
+        w2_words = keep.tile([P, GROUPS2, WIDTH], U32, align_bytes=DMA_ALIGN)
         for g in range(GROUPS2):
             nc.sync.dma_start(out=w2_words[:, g, :].bitcast(I32), in_=w2_dram[:, g, :])
         layer1_groups(range(PAIR * (PAIRS - W1_BUFS), PAIR * W1_BUFS))
@@ -324,7 +325,7 @@ def tile_gaussianrenderer_k_kernel(
         )
         inv_norm = keep.tile([P, GAUSS], F32)
         nc.scalar.activation(out=inv_norm[:], in_=norm_sq[:], func=ACT.Abs_reciprocal_sqrt)
-        result = keep.tile([P, GAUSS, CHANNELS], F32)
+        result = keep.tile([P, GAUSS, CHANNELS], F32, align_bytes=DMA_ALIGN)
         nc.vector.tensor_scalar(
             out=result[:, :, 11:16],
             in0=f_rgb[:],

from contextlib import ExitStack

import concourse.masks as masks
import concourse.mybir as mybir

F32 = mybir.dt.float32
BF16 = mybir.dt.bfloat16
I32 = mybir.dt.int32
U32 = mybir.dt.uint32
U8 = mybir.dt.uint8
FP8X4 = mybir.dt.float8_e4m3fn_x4
ALU = mybir.AluOpType
ACT = mybir.ActivationFunctionType

P = 128
PACK = 4
K_PASS = P * PACK
D_IN = 16384
WIDTH = 1024
N_PASS = 512
HALVES = WIDTH // N_PASS
GROUPS1 = D_IN // K_PASS
GROUPS2 = WIDTH // K_PASS
CHANNELS = 16
GAUSS = WIDTH // CHANNELS
GAUSS_HALF = GAUSS // HALVES
GAUSS_FIRST = 48

X_CHUNKS = 4
X_CHUNK_GROUPS = GROUPS1 // X_CHUNKS
BANK_GROUPS = 2
LATE = 2
EARLY = GROUPS1 - LATE
PAIR = 2
PAIRS = EARLY // PAIR
W1_BUFS = 13
SHARED = 4
SLOTS = GROUPS1 // SHARED
DMA_ALIGN = 256
QUADS = 4
PLANE_ROWS = 4
DUMMIES = 2
PIECES = 4
PIECE = N_PASS // PIECES

FLOPS = 2 * P * D_IN * WIDTH + 2 * P * WIDTH * WIDTH


def tile_gaussianrenderer_k_kernel(
    tc, xyzs, latents, W1_words, W1_scales, b1, W2_words, W2_scales, b2, out
):
    nc = tc.nc

    x_dram = latents.rearrange("b n d -> (b n) d")
    xyz_dram = xyzs.rearrange("b n c -> (b n) c")
    w1_dram = W1_words.rearrange("g p n t -> p g (n t)").bitcast(I32)
    w2_dram = W2_words.rearrange("g p n t -> p g (n t)").bitcast(I32)
    w2_scale_dram = W2_scales.bitcast(F32)
    out_dram = out.rearrange("b (n q) c -> (b n) (q c)", q=GAUSS)

    with ExitStack() as ctx:
        ctx.enter_context(tc.manual_schedule())
        keep = ctx.enter_context(tc.tile_pool(name="keep", bufs=1))
        x_pool = ctx.enter_context(tc.tile_pool(name="x", bufs=X_CHUNKS))
        w1_pool = ctx.enter_context(tc.tile_pool(name="w1", bufs=W1_BUFS))
        stage = ctx.enter_context(tc.tile_pool(name="stage", bufs=4))
        tail = ctx.enter_context(tc.tile_pool(name="tail", bufs=2))
        sums = ctx.enter_context(tc.psum_pool(name="sums", bufs=1))
        turn = ctx.enter_context(tc.psum_pool(name="turn", bufs=4))

        ones = keep.tile([P, P], BF16)
        nc.vector.memset(ones[:], 1.0)
        w1_planes = keep.tile([P, SLOTS, WIDTH], U8, align_bytes=DMA_ALIGN)
        nc.vector.memset(w1_planes[:].bitcast(I32), 0)
        w2_planes = keep.tile([P, WIDTH], U8, align_bytes=DMA_ALIGN)
        nc.vector.memset(w2_planes[:].bitcast(I32), 0)
        bias_rows = keep.tile([P, 2 * WIDTH], BF16)
        ident_f32 = keep.tile([P, P], F32)
        masks.make_identity(nc, ident_f32[:])

        for r in range(PLANE_ROWS):
            for quad in range(QUADS):
                nc.gpsimd.dma_start(
                    out=w1_planes[32 * quad + r : 32 * quad + 4 * SHARED : 4, :, :].bitcast(F32),
                    in_=W1_scales[:, 4 * quad + r, :]
                    .rearrange("(s j) n -> j s n", j=SHARED)
                    .bitcast(F32),
                )

        for quad in range(QUADS):
            nc.gpsimd.dma_start(
                out=w2_planes[32 * quad : 32 * quad + 4 * GROUPS2, :].bitcast(F32),
                in_=w2_scale_dram[:, 4 * quad : 4 * quad + 4, :],
            )

        x_chunks = []
        chunk_cols = X_CHUNK_GROUPS * K_PASS
        for c in range(X_CHUNKS):
            x_sb = x_pool.tile([P, chunk_cols], BF16, align_bytes=DMA_ALIGN)
            nc.sync.dma_start(out=x_sb[:], in_=x_dram[:, c * chunk_cols : (c + 1) * chunk_cols])
            x_chunks.append(x_sb)

        w1_pairs = []

        def load_w1_pair():
            w1_sb = w1_pool.tile([P, PAIR, WIDTH], U32, align_bytes=DMA_ALIGN)
            g0 = PAIR * len(w1_pairs)
            nc.sync.dma_start(out=w1_sb[:].bitcast(I32), in_=w1_dram[:, g0 : g0 + PAIR, :])
            w1_pairs.append(w1_sb)

        for n in range(W1_BUFS):
            load_w1_pair()

        warm = keep.tile([P, 1], F32)
        nc.scalar.activation(out=warm[:], in_=ones[:, 0:1], func=ACT.Silu)

        x_codes = keep.tile([P, GROUPS1, P], U32, align_bytes=64)
        x_scales = keep.tile([P, GROUPS1, P], U8, align_bytes=64)
        for bank in range(GROUPS1 // BANK_GROUPS):
            g0 = bank * BANK_GROUPS
            x_turned = turn.tile([P, BANK_GROUPS * 2, P], F32, tag="turn")
            for gi in range(BANK_GROUPS):
                x_words = x_chunks[(g0 + gi) // X_CHUNK_GROUPS][:].bitcast(F32)
                w0 = ((g0 + gi) % X_CHUNK_GROUPS) * (K_PASS // 2)
                for u in range(2):
                    nc.tensor.transpose(
                        x_turned[:, 2 * gi + u, :],
                        x_words[:, w0 + u : w0 + K_PASS // 2 : 2],
                        ident_f32[:],
                    )
            x_grouped = stage.tile([P, BANK_GROUPS * K_PASS], BF16, align_bytes=64)
            nc.scalar.copy(
                out=x_grouped[:].bitcast(F32).rearrange("p (g r u) -> p g r u", g=BANK_GROUPS, u=2),
                in_=x_turned[:].rearrange("p (g u) r -> p g r u", u=2),
            )
            nc.vector.quantize_mx(
                out=x_codes[:, g0 : g0 + BANK_GROUPS, :].rearrange("p g r -> p (g r)").bitcast(FP8X4),
                scales=x_scales[:, g0 : g0 + BANK_GROUPS, :].rearrange("p g r -> p (g r)"),
                in_=x_grouped[:],
            )

        nc.vector.memset(bias_rows[:], 0.0)
        nc.scalar.dma_start(out=bias_rows[0:1, 0:WIDTH], in_=b1.unsqueeze(0))
        nc.scalar.dma_start(out=bias_rows[0:1, WIDTH : 2 * WIDTH], in_=b2.unsqueeze(0))
        xyz_bf16 = keep.tile([P, 3], BF16)
        nc.scalar.dma_start(out=xyz_bf16[:], in_=xyz_dram)

        h_sums = [sums.tile([P, N_PASS], F32, name="h_sum%d" % half) for half in range(HALVES)]

        def w1_columns(g, cols):
            if g < EARLY:
                return w1_pairs[g // PAIR][:, g % PAIR, cols]
            return w1_late[:, g - EARLY, cols]

        def layer1_pass(g, half):
            cols = slice(half * N_PASS, (half + 1) * N_PASS)
            nc.tensor.matmul_mx(
                out=h_sums[half][:],
                lhsT=x_codes[:, g, :].bitcast(FP8X4),
                lhsT_scale=x_scales[:, g, :],
                rhs=w1_columns(g, cols).bitcast(FP8X4),
                rhs_scale=w1_planes[4 * (g % SHARED) : P, g // SHARED, cols],
                start=(g == 0),
                stop=(g == GROUPS1 - 1),
            )

        def layer1_groups(groups):
            for g in groups:
                for half in range(HALVES):
                    layer1_pass(g, half)

        for n in range(PAIRS - W1_BUFS):
            layer1_groups(range(PAIR * n, PAIR * (n + 1)))
            load_w1_pair()
        w1_late = keep.tile([P, LATE, WIDTH], U32, align_bytes=DMA_ALIGN)
        for g0, g1, half in ((EARLY, GROUPS1, 0), (EARLY, GROUPS1 - 1, 1), (GROUPS1 - 1, GROUPS1, 1)):
            cols = slice(half * N_PASS, (half + 1) * N_PASS)
            nc.sync.dma_start(
                out=w1_late[:, g0 - EARLY : g1 - EARLY, cols].bitcast(I32), in_=w1_dram[:, g0:g1, cols]
            )
        w2_words = keep.tile([P, GROUPS2, WIDTH], U32, align_bytes=DMA_ALIGN)
        for g in range(GROUPS2):
            nc.sync.dma_start(out=w2_words[:, g, :].bitcast(I32), in_=w2_dram[:, g, :])
        layer1_groups(range(PAIR * (PAIRS - W1_BUFS), PAIR * W1_BUFS))

        b1_all = keep.tile([P, WIDTH], F32)
        b2_all = keep.tile([P, GAUSS, CHANNELS], F32)
        for half in range(HALVES):
            spread = turn.tile([P, N_PASS], F32, tag="turn")
            nc.tensor.matmul(
                out=spread[:],
                lhsT=ones[:],
                rhs=bias_rows[:, half * N_PASS : (half + 1) * N_PASS],
                start=True,
                stop=True,
            )
            nc.vector.tensor_copy(
                out=b1_all[:, half * N_PASS : (half + 1) * N_PASS], in_=spread[:]
            )
        for half in range(HALVES):
            spread = turn.tile([P, N_PASS], F32, tag="turn")
            nc.tensor.matmul(
                out=spread[:],
                lhsT=ones[:],
                rhs=bias_rows[:, WIDTH + half * N_PASS : WIDTH + (half + 1) * N_PASS],
                start=True,
                stop=True,
            )
            nc.vector.tensor_copy(
                out=b2_all[:, half * GAUSS_HALF : (half + 1) * GAUSS_HALF, :],
                in_=spread[:].rearrange("p (q c) -> p q c", c=CHANNELS),
            )
        nc.vector.tensor_scalar_add(out=b2_all[:, :, 11:16], in0=b2_all[:, :, 11:16], scalar1=0.5)
        xyz_shift = keep.tile([P, 3], F32)
        nc.vector.tensor_scalar_add(out=xyz_shift[:], in0=xyz_bf16[:], scalar1=0.1)

        layer1_groups(range(PAIR * W1_BUFS, EARLY))

        h_codes = keep.tile([P, GROUPS2, P], U32, align_bytes=64)
        h_scales = keep.tile([P, GROUPS2, P], U8, align_bytes=64)

        def silu_half(half):
            pre = tail.tile([P, N_PASS], F32)
            h_bf16 = tail.tile([P, 2, P, 2], BF16)
            for piece in range(PIECES):
                some = slice(piece * PIECE, (piece + 1) * PIECE)
                nc.vector.tensor_tensor(
                    out=pre[:, some],
                    in0=h_sums[half][:, some],
                    in1=b1_all[:, half * N_PASS + piece * PIECE : half * N_PASS + (piece + 1) * PIECE],
                    op=ALU.add,
                )
                nc.scalar.activation(
                    out=h_bf16[:, :, piece * P // PIECES : (piece + 1) * P // PIECES, :],
                    in_=pre[:, some].rearrange("p (i u e) -> p u i e", u=2, e=2),
                    func=ACT.Silu,
                )
            return h_bf16

        def turn_half(h_bf16):
            turned = turn.tile([P, 2, P], F32, tag="turn")
            for u in range(2):
                nc.tensor.transpose(
                    turned[:, u, :],
                    h_bf16[:, u, :, :].rearrange("p i e -> p (i e)").bitcast(F32),
                    ident_f32[:],
                )
            return turned

        def group_half(half, turned):
            h_grouped = tail.tile([P, N_PASS], BF16, align_bytes=64)
            copy = nc.vector.tensor_copy if half == 0 else nc.scalar.copy
            copy(
                out=h_grouped[:].bitcast(F32).rearrange("p (r u) -> p r u", u=2),
                in_=turned[:].rearrange("p u r -> p r u"),
            )
            return h_grouped

        def quantise_half(half, h_grouped):
            nc.vector.quantize_mx(
                out=h_codes[:, half, :].bitcast(FP8X4),
                scales=h_scales[:, half, :],
                in_=h_grouped[:],
            )

        h_halves = []
        for half in range(HALVES):
            for g in range(EARLY, GROUPS1):
                layer1_pass(g, half)
            h_halves.append(silu_half(half))
        turned = turn_half(h_halves[0])
        for dummy in range(DUMMIES):
            idle = turn.tile([P, N_PASS], F32, tag="turn")
            nc.tensor.matmul(
                out=idle[:], lhsT=ones[:], rhs=bias_rows[:, 0:N_PASS], start=True, stop=True
            )
        quantise_half(0, group_half(0, turned))
        quantise_half(1, group_half(1, turn_half(h_halves[1])))

        f_sums = [sums.tile([P, N_PASS], F32, name="f_sum%d" % half) for half in range(HALVES)]
        for g in range(GROUPS2):
            for half in range(HALVES):
                cols = slice(half * N_PASS, (half + 1) * N_PASS)
                nc.tensor.matmul_mx(
                    out=f_sums[half][:],
                    lhsT=h_codes[:, g, :].bitcast(FP8X4),
                    lhsT_scale=h_scales[:, g, :],
                    rhs=w2_words[:, g, cols].bitcast(FP8X4),
                    rhs_scale=w2_planes[4 * g : P, cols],
                    start=(g == 0),
                    stop=(g == GROUPS2 - 1),
                )

        def dense(chans):
            return keep.tile([P, GAUSS, chans.stop - chans.start], F32, name="f%d" % chans.start)

        def add_bias(summed, chans, half):
            some = slice(half * GAUSS_HALF, (half + 1) * GAUSS_HALF)
            nc.vector.tensor_tensor(
                out=summed[:, some, :],
                in0=f_sums[half][:].rearrange("p (q c) -> p q c", c=CHANNELS)[:, :, chans],
                in1=b2_all[:, some, chans],
                op=ALU.add,
            )

        sigmoid_chans, rot_chans, rgb_chans = slice(0, 7), slice(7, 11), slice(11, CHANNELS)
        f_sigmoid, f_rot, f_rgb = dense(sigmoid_chans), dense(rot_chans), dense(rgb_chans)
        for half in range(HALVES):
            add_bias(f_sigmoid, sigmoid_chans, half)
        tanhs = keep.tile([P, GAUSS, 7], F32)
        for half in range(HALVES):
            some = slice(half * GAUSS_HALF, (half + 1) * GAUSS_HALF)
            nc.scalar.activation(
                out=tanhs[:, some, :], in_=f_sigmoid[:, some, :], func=ACT.Tanh, scale=0.5
            )
        for half in range(HALVES):
            add_bias(f_rot, rot_chans, half)
        add_bias(f_rgb, rgb_chans, 0)
        squares = keep.tile([P, GAUSS, 4], F32)
        nc.vector.tensor_tensor(out=squares[:], in0=f_rot[:], in1=f_rot[:], op=ALU.mult)
        add_bias(f_rgb, rgb_chans, 1)
        norm_sq = keep.tile([P, GAUSS], F32)
        nc.vector.tensor_reduce(
            out=norm_sq[:], in_=squares[:], axis=mybir.AxisListType.X, op=ALU.add
        )
        inv_norm = keep.tile([P, GAUSS], F32)
        nc.scalar.activation(out=inv_norm[:], in_=norm_sq[:], func=ACT.Abs_reciprocal_sqrt)
        result = keep.tile([P, GAUSS, CHANNELS], F32, align_bytes=DMA_ALIGN)
        nc.vector.tensor_scalar(
            out=result[:, :, 11:16],
            in0=f_rgb[:],
            scalar1=0.0,
            scalar2=1.0,
            op0=ALU.max,
            op1=ALU.min,
        )
        nc.vector.scalar_tensor_tensor(
            out=result[:, :, 0:3],
            in0=tanhs[:, :, 0:3],
            scalar=0.1,
            in1=xyz_shift[:].unsqueeze(1).to_broadcast([P, GAUSS, 3]),
            op0=ALU.mult,
            op1=ALU.add,
        )
        for q0, q1 in ((0, GAUSS_FIRST), (GAUSS_FIRST, GAUSS)):
            some = slice(q0, q1)
            nc.scalar.activation(
                out=result[:, some, 3:4], in_=tanhs[:, some, 3:4], func=ACT.Copy, scale=0.5, bias=0.5
            )
            nc.scalar.activation(
                out=result[:, some, 4:7], in_=tanhs[:, some, 4:7], func=ACT.Copy, scale=0.01, bias=0.01
            )
            nc.vector.scalar_tensor_tensor(
                out=result[:, some, 7:11],
                in0=inv_norm[:, some].unsqueeze(2).to_broadcast([P, q1 - q0, 4]),
                scalar=1.0e12,
                in1=f_rot[:, some, :],
                op0=ALU.min,
                op1=ALU.mult,
            )
            nc.sync.dma_start(
                out=out_dram[:, q0 * CHANNELS : q1 * CHANNELS],
                in_=result[:, some, :].rearrange("p q c -> p (q c)"),
            )
